import numpy as np
import ml_dtypes


def mxq(x, axis, fmt="e4m3"):
    dtype, down = {"e4m3": (ml_dtypes.float8_e4m3fn, 7), "e5m2": (ml_dtypes.float8_e5m2, 14)}[fmt]
    v = np.moveaxis(np.asarray(x, np.float32).astype(ml_dtypes.bfloat16).astype(np.float64), axis, -1)
    blocks = v.reshape(v.shape[:-1] + (-1, 32))
    amax = np.abs(blocks).max(-1, keepdims=True)
    byte = np.maximum(np.where(amax > 0, np.frexp(amax)[1] - 1 + 127, 0) - down, 1)
    scale = np.exp2(byte - 127.0)
    codes = (blocks / scale).astype(np.float32).astype(dtype).astype(np.float64)
    return np.moveaxis((codes * scale).reshape(v.shape), -1, axis)


WIDE = False


def mx_kscale(k):
    if not WIDE:
        return np.ones(k)
    levels = np.array([10, -10, 5, -5, 0])
    a = np.random.permutation(np.resize(levels, k // 512 * 4)).reshape(k // 512, 4)
    idx = np.arange(k)
    return np.exp2(a[idx // 512, idx % 128 // 32])


BF16 = ml_dtypes.bfloat16


def bf(x):
    return np.asarray(x, np.float32).astype(BF16)


def f64(x):
    return np.asarray(x).astype(np.float64)


T, H, NQ, NKV, HD = 512, 2048, 32, 2, 128
RD = HD // 2
QS, KS = NQ * HD, NKV * HD
OUT = QS + 2 * KS


def extract_rope(x):
    r = x[..., :RD]
    r = r.reshape(*r.shape[:-1], RD // 2, 2)
    return np.swapaxes(r, -2, -1).reshape(*x.shape[:-1], RD)


def fill_rope(x, rope):
    r = rope.reshape(*rope.shape[:-1], 2, RD // 2)
    r = np.swapaxes(r, -2, -1).reshape(*rope.shape)
    return np.concatenate([r, x[..., RD:]], axis=-1)


def rotate_half(x):
    half = x.shape[-1] // 2
    return np.concatenate([-x[..., half:], x[..., :half]], axis=-1)


def setup_inputs():
    s = mx_kscale(H)
    ang = np.random.uniform(0.0, 2.0 * np.pi, (T, RD))
    return {'hidden_states': bf(np.random.standard_normal((T, H)) * s),
            'cos': bf(np.cos(ang)), 'sin': bf(np.sin(ang)),
            'W_qkv': bf(np.random.standard_normal((H, OUT)) / np.sqrt(H) / s[:, None]),
            'b_qkv': bf(np.random.standard_normal(OUT) * 0.3)}


def reference(hidden_states, cos, sin, W_qkv, b_qkv):
    qkv = (mxq(f64(hidden_states), 1, 'e4m3') @ mxq(f64(W_qkv), 0, 'e4m3')) + f64(b_qkv)
    q = qkv[:, :QS].reshape(T, NQ, HD)
    k = qkv[:, QS:QS + KS].reshape(T, NKV, HD)
    v = qkv[:, QS + KS:].reshape(T, NKV, HD)
    cos_b = f64(cos)[:, None, :]
    sin_b = f64(sin)[:, None, :]
    q_r = extract_rope(q)
    k_r = extract_rope(k)
    q_r = q_r * cos_b + rotate_half(q_r) * sin_b
    k_r = k_r * cos_b + rotate_half(k_r) * sin_b
    q = fill_rope(q, q_r)
    k = fill_rope(k, k_r)
    return q, k, v

@@ -1,0 +1,270 @@
+from contextlib import ExitStack
+
+import concourse.mybir as mybir
+from concourse.masks import make_identity
+
+F32 = mybir.dt.float32
+BF16 = mybir.dt.bfloat16
+U32 = mybir.dt.uint32
+U8 = mybir.dt.uint8
+FP8X4 = mybir.dt.float8_e4m3fn_x4
+ADD = mybir.AluOpType.add
+MULT = mybir.AluOpType.mult
+
+P = 128
+T, H, NQ, NKV, HD = 512, 2048, 32, 2, 128
+QS, KS = NQ * HD, NKV * HD
+OUT = QS + 2 * KS
+PASSES = H // 512
+TT = T // P
+HALF = HD // 2
+ROPE_HEADS = NQ + NKV
+FLOPS = 2 * T * H * OUT
+
+CHUNKS = [(0, 4), (4, 8), (12, 8), (20, 8), (28, 8)]
+VECTOR_PIECES = {0: {(0, 0), (1, 0), (2, 0), (3, 0)}, 1: {(0, 0), (1, 0), (2, 0)}, 2: {(0, 0), (1, 0), (2, 0)},
+                 3: {(0, 0), (1, 0), (2, 0)}, 4: {(0, 0), (1, 0), (2, 0)}}
+
+
+def split_widths(width):
+    parts = []
+    start = 0
+    for n in (512, 256, 128):
+        while width - start >= n:
+            parts.append((start, n))
+            start += n
+    return parts
+
+
+def tile_selfattention_pa_kernel(tc, hidden_states, cos, sin, W_qkv, b_qkv, out_0, out_1, out_2):
+    nc = tc.nc
+    q_out = out_0.rearrange("t h d -> t (h d)")
+    k_out = out_1.rearrange("t h d -> t (h d)")
+    v_out = out_2.rearrange("t h d -> t (h d)")
+    with ExitStack() as ctx:
+        const = ctx.enter_context(tc.tile_pool(name="const", bufs=1))
+        rawp = ctx.enter_context(tc.tile_pool(name="rawp", bufs=10))
+        grp = ctx.enter_context(tc.tile_pool(name="grp", bufs=3))
+        wq = ctx.enter_context(tc.tile_pool(name="wq", bufs=2))
+        zp = ctx.enter_context(tc.tile_pool(name="zp", bufs=6))
+        uvp = ctx.enter_context(tc.tile_pool(name="uvp", bufs=12))
+        psum = ctx.enter_context(tc.psum_pool(name="psum", bufs=1))
+
+        ident = const.tile([P, P], F32, name="ident")
+        make_identity(nc, ident[:])
+        swp = const.tile([P, P], F32, name="swp")
+        cosn = const.tile([P, TT, 64], BF16, name="cosn")
+        sinn = const.tile([P, TT, 64], BF16, name="sinn")
+        brow = const.tile([P, P], BF16, name="brow")
+        browf = const.tile([P, P], F32, name="browf")
+        b_rope = const.tile([P, ROPE_HEADS // 2], F32, name="b_rope")
+        cos_t = const.tile([P, T], BF16, name="cos_t")
+        sin_t = const.tile([P, T], BF16, name="sin_t")
+        bias = const.tile([P, OUT], BF16, name="bias")
+        hcodes = const.tile([P, PASSES, T], U32, name="hcodes", align_bytes=64)
+        hscales = const.tile([P, PASSES, T], U8, name="hscales", align_bytes=64)
+
+        raws = {}
+
+        def load_chunk(i):
+            h0, nh = CHUNKS[i]
+            for c in range(PASSES):
+                raw = rawp.tile([P, 4, nh * HD], BF16, name="raw%d_%d" % (i, c), tag="raw")
+                nc.sync.dma_start(
+                    out=raw[:],
+                    in_=W_qkv[512 * c : 512 * (c + 1), h0 * HD : (h0 + nh) * HD].rearrange("(p j) w -> p j w", j=4),
+                )
+                raws[(i, c)] = raw
+
+        nc.vector.memset(brow[:], 0.0)
+        nc.scalar.dma_start(out=cosn[:], in_=cos.rearrange("(t p) d -> p t d", p=P))
+        nc.scalar.dma_start(out=sinn[:], in_=sin.rearrange("(t p) d -> p t d", p=P))
+        nc.scalar.dma_start(
+            out=brow[0 : ROPE_HEADS // 2, :].rearrange("r (h d) -> r h d", h=2),
+            in_=b_qkv[0 : ROPE_HEADS * HD].rearrange("(r h s d) -> r h s d", h=2, s=2, d=HALF)[:, :, 0, :],
+        )
+        load_chunk(0)
+        xs = []
+        for t in range(TT):
+            x_sb = zp.tile([P, H], BF16, name="x%d" % t, tag="z")
+            nc.sync.dma_start(out=x_sb[:], in_=hidden_states[P * t : P * (t + 1), :])
+            xs.append(x_sb)
+        nc.scalar.dma_start(out=bias[:], in_=b_qkv.partition_broadcast(P))
+        load_chunk(1)
+
+        idv = ident[:].rearrange("p (m e) -> p m e", e=2)
+        swv = swp[:].rearrange("p (m e) -> p m e", e=2)
+        for e in range(2):
+            nc.vector.tensor_copy(out=swv[:, :, e], in_=idv[:, :, 1 - e])
+
+        cn = uvp.tile([P, TT, 2, 32, 2], F32, name="cn", tag="uv")
+        sn = uvp.tile([P, TT, 2, 32, 2], F32, name="sn", tag="uv")
+        nc.vector.tensor_scalar_mul(out=sinn[:, :, 0:32], in0=sinn[:, :, 0:32], scalar1=-1.0)
+        for e in range(2):
+            nc.vector.tensor_copy(
+                out=cn[:, :, :, :, e],
+                in_=cosn[:, :, 32 * e : 32 * (e + 1)].unsqueeze(2).to_broadcast([P, TT, 2, 32]),
+            )
+            nc.vector.tensor_copy(
+                out=sn[:, :, :, :, e],
+                in_=sinn[:, :, 32 * (1 - e) : 32 * (2 - e)].unsqueeze(2).to_broadcast([P, TT, 2, 32]),
+            )
+        nc.vector.tensor_copy(out=browf[:], in_=brow[:])
+        for src, dst in ((cn, cos_t), (sn, sin_t)):
+            tb = psum.tile([P, T], F32, name="tb", tag="y", bufs=2)
+            for t in range(TT):
+                nc.tensor.transpose(
+                    tb[:, P * t : P * (t + 1)], src[:, t].rearrange("p h j e -> p (h j e)"), ident[:]
+                )
+            nc.vector.tensor_copy(out=dst[:], in_=tb[:])
+        pb = psum.tile([P, T], F32, name="pb", tag="y", bufs=2)
+        nc.tensor.transpose(pb[:, 0:P], browf[:], ident[:])
+        nc.vector.tensor_copy(out=b_rope[:], in_=pb[:, 0 : ROPE_HEADS // 2])
+
+        hgs = []
+        for cp in range(2):
+            hg = grp.tile([P, 2, T, 4], BF16, name="hg%d" % cp, tag="grouped", align_bytes=64)
+            hgs.append(hg)
+        for t in range(TT):
+            xw = xs[t][:].bitcast(F32)
+            for cp in range(2):
+                xt = psum.tile([P, 2, 2, P], F32, name="xt%d_%d" % (t, cp), tag="y", bufs=2)
+                for ci in range(2):
+                    c = 2 * cp + ci
+                    for u in range(2):
+                        nc.tensor.transpose(xt[:, ci, u, :], xw[:, 256 * c + u : 256 * (c + 1) : 2], ident[:])
+                nc.scalar.copy(
+                    out=hgs[cp][:].bitcast(F32)[:, :, P * t : P * (t + 1), :],
+                    in_=xt[:].rearrange("p c u r -> p c r u"),
+                )
+        for c in range(PASSES):
+            nc.vector.quantize_mx(
+                out=hcodes[:, c, :].bitcast(FP8X4),
+                scales=hscales[:, c, :],
+                in_=hgs[c // 2][:, c % 2].rearrange("p r j -> p (r j)"),
+            )
+
+        codes = {}
+
+        def regroup(i):
+            h0, nh = CHUNKS[i]
+            w = nh * HD
+            nr = min(h0 + nh, ROPE_HEADS) - h0
+            rw = nr * HALF
+            wc = wq.tile([P, PASSES, w], U32, name="wc%d" % i, tag="wc", align_bytes=64)
+            ws = wq.tile([P, PASSES, w], U8, name="ws%d" % i, tag="ws", align_bytes=64)
+            codes[i] = (wc, ws)
+            for c in range(PASSES):
+                raw = raws[(i, c)]
+                g = grp.tile([P, w, 4], BF16, name="g%d_%d" % (i, c), tag="grouped", align_bytes=64)
+                halves = raw[:, :, 0 : nr * HD].rearrange("p t (h s c i) -> p s h c t i", s=2, c=16, i=4)
+                pieces = []
+                for s in range(2):
+                    pieces.append(
+                        (g[:, s * rw : (s + 1) * rw, :].rearrange("p (h c i) t -> p h c t i", c=16, i=4), halves[:, s])
+                    )
+                if nr < nh:
+                    pieces.append(
+                        (
+                            g[:, 2 * rw : w, :].rearrange("p (c i) t -> p c t i", i=4),
+                            raw[:, :, nr * HD : w].rearrange("p t (c i) -> p c t i", i=4),
+                        )
+                    )
+                for s, (dst, src) in enumerate(pieces):
+                    if (c, s) in VECTOR_PIECES[i]:
+                        nc.vector.tensor_copy(out=dst, in_=src)
+                    else:
+                        nc.scalar.copy(out=dst, in_=src)
+                nc.vector.quantize_mx(
+                    out=wc[:, c, :].bitcast(FP8X4),
+                    scales=ws[:, c, :],
+                    in_=g[:].rearrange("p w j -> p (w j)"),
+                )
+
+        bias_h = bias[:].rearrange("p (h d) -> p h d", d=HD)
+        regroup(0)
+        for i, (h0, nh) in enumerate(CHUNKS):
+            if i + 2 < len(CHUNKS):
+                load_chunk(i + 2)
+            if i + 1 < len(CHUNKS):
+                regroup(i + 1)
+            w = nh * HD
+            nr = min(h0 + nh, ROPE_HEADS) - h0
+            rw = nr * HALF
+            wc, ws = codes[i]
+            us = []
+            for r in range(nr // 2):
+                cols = slice(P * r, P * (r + 1))
+                acc_b = psum.tile([P, T], F32, name="accb%d_%d" % (i, r), tag="accb", bufs=4)
+                for c in range(PASSES):
+                    nc.tensor.matmul_mx(
+                        out=acc_b[:],
+                        lhsT=wc[:, c, cols].bitcast(FP8X4),
+                        lhsT_scale=ws[:, c, cols],
+                        rhs=hcodes[:, c, :].bitcast(FP8X4),
+                        rhs_scale=hscales[:, c, :],
+                        start=(c == 0),
+                        stop=(c == PASSES - 1),
+                    )
+                gr = h0 // 2 + r
+                uu = uvp.tile([P, T], F32, name="uu%d_%d" % (i, r), tag="uv")
+                vv = uvp.tile([P, T], F32, name="vv%d_%d" % (i, r), tag="uv")
+                nc.vector.scalar_tensor_tensor(
+                    out=uu[:], in0=acc_b[:], scalar=b_rope[:, gr : gr + 1], in1=cos_t[:], op0=ADD, op1=MULT
+                )
+                nc.vector.scalar_tensor_tensor(
+                    out=vv[:], in0=acc_b[:], scalar=b_rope[:, gr : gr + 1], in1=sin_t[:], op0=ADD, op1=MULT
+                )
+                us.append((uu, vv))
+            zs = []
+            for t in range(TT):
+                z = zp.tile([P, w], F32, name="z%d_%d" % (i, t), tag="z")
+                zs.append(z)
+                zh = z[:].rearrange("p (h d) -> p h d", d=HD)
+                for g0, n in split_widths(w - rw):
+                    cols = slice(rw + g0, rw + g0 + n)
+                    acc_a = psum.tile([P, 512], F32, name="acca%d_%d_%d" % (i, t, g0), tag="acca", bufs=2)
+                    for c in range(PASSES):
+                        nc.tensor.matmul_mx(
+                            out=acc_a[:, 0:n],
+                            lhsT=hcodes[:, c, P * t : P * (t + 1)].bitcast(FP8X4),
+                            lhsT_scale=hscales[:, c, P * t : P * (t + 1)],
+                            rhs=wc[:, c, cols].bitcast(FP8X4),
+                            rhs_scale=ws[:, c, cols],
+                            start=(c == 0),
+                            stop=(c == PASSES - 1),
+                        )
+                    if g0 < rw:
+                        b0, b1 = g0 // HALF, min(g0 + n, rw) // HALF
+                        nc.vector.tensor_tensor(
+                            out=zh[:, b0:b1, HALF:HD],
+                            in0=acc_a[:, 0 : (b1 - b0) * HALF].rearrange("p (h d) -> p h d", d=HALF),
+                            in1=bias_h[:, h0 + b0 : h0 + b1, HALF:HD],
+                            op=ADD,
+                        )
+                    if g0 + n > rw:
+                        v0 = max(g0, rw)
+                        zc = slice(v0 + rw, g0 + n + rw)
+                        nc.vector.tensor_tensor(
+                            out=z[:, zc],
+                            in0=acc_a[:, v0 - g0 : n],
+                            in1=bias[:, h0 * HD + v0 + rw : h0 * HD + g0 + n + rw],
+                            op=ADD,
+                        )
+            for t in range(TT):
+                z = zs[t]
+                zh = z[:].rearrange("p (h d) -> p h d", d=HD)
+                toks = slice(P * t, P * (t + 1))
+                y = psum.tile([P, 512], F32, name="y%d_%d" % (i, t), tag="y", bufs=2)
+                for r, (uu, vv) in enumerate(us):
+                    cols = slice(P * r, P * (r + 1))
+                    nc.tensor.matmul(out=y[:, cols], lhsT=uu[:, toks], rhs=ident[:], start=True, stop=False, is_transpose=True)
+                    nc.tensor.matmul(out=y[:, cols], lhsT=vv[:, toks], rhs=swp[:], start=False, stop=True, is_transpose=True)
+                nc.scalar.copy(out=zh[:, 0:nr, 0:HALF], in_=y[:, 0:rw].rearrange("p (h d) -> p h d", d=HALF))
+                rows = slice(P * t, P * (t + 1))
+                c0 = h0 * HD
+                qw = min(c0 + w, QS) - c0
+                nc.sync.dma_start(out=q_out[rows, c0 : c0 + qw], in_=z[:, 0:qw])
+                if qw < w:
+                    nc.sync.dma_start(out=k_out[rows, :], in_=z[:, qw : qw + KS])
+                    nc.sync.dma_start(out=v_out[rows, :], in_=z[:, qw + KS : qw + 2 * KS])

@@ -21,9 +21,13 @@ HALF = HD // 2
 ROPE_HEADS = NQ + NKV
 FLOPS = 2 * T * H * OUT
 
-CHUNKS = [(0, 4), (4, 8), (12, 8), (20, 8), (28, 8)]
-VECTOR_PIECES = {0: {(0, 0), (1, 0), (2, 0), (3, 0)}, 1: {(0, 0), (1, 0), (2, 0)}, 2: {(0, 0), (1, 0), (2, 0)},
-                 3: {(0, 0), (1, 0), (2, 0)}, 4: {(0, 0), (1, 0), (2, 0)}}
+LOADS = [(0, 4), (4, 8), (12, 8), (20, 8), (28, 8)]
+UNITS = [(0, 4, 0), (4, 8, 1), (12, 8, 2), (20, 8, 3), (28, 4, 4), (32, 4, 4)]
+VSHARE = [[4, 4, 4, 4], [8, 8, 8, 8], [4, 4, 4, 4], [4, 4, 4, 4], [4, 4, 4, 4], [0, 0, 0, 0]]
+HEAD_LOADS = ["hs", 4, "b0", 4, 2, "bias"]
+RAW_SLOTS = 10
+EARLY = 0
+PIN = False
 
 
 def split_widths(width):
@@ -41,13 +45,16 @@ def tile_selfattention_pa_kernel(tc, hidden_states, cos, sin, W_qkv, b_qkv, out_
     q_out = out_0.rearrange("t h d -> t (h d)")
     k_out = out_1.rearrange("t h d -> t (h d)")
     v_out = out_2.rearrange("t h d -> t (h d)")
+    n_units = len(UNITS)
     with ExitStack() as ctx:
+        if PIN:
+            ctx.enter_context(tc.manual_schedule())
         const = ctx.enter_context(tc.tile_pool(name="const", bufs=1))
-        rawp = ctx.enter_context(tc.tile_pool(name="rawp", bufs=10))
-        grp = ctx.enter_context(tc.tile_pool(name="grp", bufs=3))
+        rawp = ctx.enter_context(tc.tile_pool(name="rawp", bufs=RAW_SLOTS))
+        grp = ctx.enter_context(tc.tile_pool(name="grp", bufs=4))
         wq = ctx.enter_context(tc.tile_pool(name="wq", bufs=2))
-        zp = ctx.enter_context(tc.tile_pool(name="zp", bufs=6))
-        uvp = ctx.enter_context(tc.tile_pool(name="uvp", bufs=12))
+        zp = ctx.enter_context(tc.tile_pool(name="zp", bufs=2))
+        uvp = ctx.enter_context(tc.tile_pool(name="uvp", bufs=6))
         psum = ctx.enter_context(tc.psum_pool(name="psum", bufs=1))
 
         ident = const.tile([P, P], F32, name="ident")
@@ -63,18 +70,22 @@ def tile_selfattention_pa_kernel(tc, hidden_states, cos, sin, W_qkv, b_qkv, out_
         bias = const.tile([P, OUT], BF16, name="bias")
         hcodes = const.tile([P, PASSES, T], U32, name="hcodes", align_bytes=64)
         hscales = const.tile([P, PASSES, T], U8, name="hscales", align_bytes=64)
+        bias_h = bias[:].rearrange("p (h d) -> p h d", d=HD)
 
         raws = {}
+        pending = [(j, c) for j in range(len(LOADS)) for c in range(PASSES)]
 
-        def load_chunk(i):
-            h0, nh = CHUNKS[i]
-            for c in range(PASSES):
-                raw = rawp.tile([P, 4, nh * HD], BF16, name="raw%d_%d" % (i, c), tag="raw")
-                nc.sync.dma_start(
-                    out=raw[:],
-                    in_=W_qkv[512 * c : 512 * (c + 1), h0 * HD : (h0 + nh) * HD].rearrange("(p j) w -> p j w", j=4),
-                )
-                raws[(i, c)] = raw
+        def load_next():
+            if not pending:
+                return
+            j, c = pending.pop(0)
+            h0, nh = LOADS[j]
+            raw = rawp.tile([P, 4, nh * HD], BF16, name="raw%d_%d" % (j, c), tag="raw")
+            nc.sync.dma_start(
+                out=raw[:],
+                in_=W_qkv[512 * c : 512 * (c + 1), h0 * HD : (h0 + nh) * HD].rearrange("(p j) w -> p j w", j=4),
+            )
+            raws[(j, c)] = raw
 
         nc.vector.memset(brow[:], 0.0)
         nc.scalar.dma_start(out=cosn[:], in_=cos.rearrange("(t p) d -> p t d", p=P))
@@ -83,14 +94,19 @@ def tile_selfattention_pa_kernel(tc, hidden_states, cos, sin, W_qkv, b_qkv, out_
             out=brow[0 : ROPE_HEADS // 2, :].rearrange("r (h d) -> r h d", h=2),
             in_=b_qkv[0 : ROPE_HEADS * HD].rearrange("(r h s d) -> r h s d", h=2, s=2, d=HALF)[:, :, 0, :],
         )
-        load_chunk(0)
-        xs = []
-        for t in range(TT):
-            x_sb = zp.tile([P, H], BF16, name="x%d" % t, tag="z")
-            nc.sync.dma_start(out=x_sb[:], in_=hidden_states[P * t : P * (t + 1), :])
-            xs.append(x_sb)
-        nc.scalar.dma_start(out=bias[:], in_=b_qkv.partition_broadcast(P))
-        load_chunk(1)
+        x_all = zp.tile([P, TT, H], BF16, name="x_all", tag="z")
+        b_cut = UNITS[0][1] * HD
+        for item in HEAD_LOADS:
+            if item == "hs":
+                for t in range(TT):
+                    nc.sync.dma_start(out=x_all[:, t, :], in_=hidden_states[P * t : P * (t + 1), :])
+            elif item == "b0":
+                nc.sync.dma_start(out=bias[:, 0:b_cut], in_=b_qkv[0:b_cut].partition_broadcast(P))
+            elif item == "bias":
+                nc.sync.dma_start(out=bias[:, b_cut:OUT], in_=b_qkv[b_cut:OUT].partition_broadcast(P))
+            else:
+                for q in range(item):
+                    load_next()
 
         idv = ident[:].rearrange("p (m e) -> p m e", e=2)
         swv = swp[:].rearrange("p (m e) -> p m e", e=2)
@@ -113,158 +129,232 @@ def tile_selfattention_pa_kernel(tc, hidden_states, cos, sin, W_qkv, b_qkv, out_
         for src, dst in ((cn, cos_t), (sn, sin_t)):
             tb = psum.tile([P, T], F32, name="tb", tag="y", bufs=2)
             for t in range(TT):
-                nc.tensor.transpose(
-                    tb[:, P * t : P * (t + 1)], src[:, t].rearrange("p h j e -> p (h j e)"), ident[:]
-                )
+                nc.tensor.transpose(tb[:, P * t : P * (t + 1)], src[:, t].rearrange("p h j e -> p (h j e)"), ident[:])
             nc.vector.tensor_copy(out=dst[:], in_=tb[:])
         pb = psum.tile([P, T], F32, name="pb", tag="y", bufs=2)
         nc.tensor.transpose(pb[:, 0:P], browf[:], ident[:])
         nc.vector.tensor_copy(out=b_rope[:], in_=pb[:, 0 : ROPE_HEADS // 2])
 
-        hgs = []
-        for cp in range(2):
-            hg = grp.tile([P, 2, T, 4], BF16, name="hg%d" % cp, tag="grouped", align_bytes=64)
-            hgs.append(hg)
-        for t in range(TT):
-            xw = xs[t][:].bitcast(F32)
+        def hidden():
+            hgs = []
             for cp in range(2):
-                xt = psum.tile([P, 2, 2, P], F32, name="xt%d_%d" % (t, cp), tag="y", bufs=2)
-                for ci in range(2):
-                    c = 2 * cp + ci
-                    for u in range(2):
-                        nc.tensor.transpose(xt[:, ci, u, :], xw[:, 256 * c + u : 256 * (c + 1) : 2], ident[:])
-                nc.scalar.copy(
-                    out=hgs[cp][:].bitcast(F32)[:, :, P * t : P * (t + 1), :],
-                    in_=xt[:].rearrange("p c u r -> p c r u"),
+                hg = grp.tile([P, 2, T, 4], BF16, name="hg%d" % cp, tag="grouped", align_bytes=64)
+                hgs.append(hg)
+            for t in range(TT):
+                xw = x_all[:, t, :].bitcast(F32)
+                for cp in range(2):
+                    xt = psum.tile([P, 2, 2, P], F32, name="xt%d_%d" % (t, cp), tag="y", bufs=2)
+                    for ci in range(2):
+                        c = 2 * cp + ci
+                        for u in range(2):
+                            nc.tensor.transpose(xt[:, ci, u, :], xw[:, 256 * c + u : 256 * (c + 1) : 2], ident[:])
+                    dst = hgs[cp][:].bitcast(F32)[:, :, P * t : P * (t + 1), :]
+                    if cp == 9:
+                        nc.vector.tensor_copy(out=dst, in_=xt[:].rearrange("p c u r -> p c r u"))
+                    else:
+                        nc.scalar.copy(out=dst, in_=xt[:].rearrange("p c u r -> p c r u"))
+            for c in range(PASSES):
+                nc.vector.quantize_mx(
+                    out=hcodes[:, c, :].bitcast(FP8X4),
+                    scales=hscales[:, c, :],
+                    in_=hgs[c // 2][:, c % 2].rearrange("p r j -> p (r j)"),
                 )
-        for c in range(PASSES):
+
+        st = {}
+
+        def rope_heads(k):
+            h0, nh, j = UNITS[k]
+            return min(h0 + nh, ROPE_HEADS) - h0
+
+        def tiles(k):
+            return rope_heads(k) // 2
+
+        def regroup(k, c):
+            h0, nh, j = UNITS[k]
+            w = nh * HD
+            nr = rope_heads(k)
+            rw = nr * HALF
+            if c == 0:
+                wc = wq.tile([P, PASSES, w], U32, name="wc%d" % k, tag="wc", align_bytes=64)
+                ws = wq.tile([P, PASSES, w], U8, name="ws%d" % k, tag="ws", align_bytes=64)
+                st[k] = {"wc": wc, "ws": ws, "g": {}, "accb": {}, "uv": {}, "y": {}, "acca": {}}
+            off = (h0 - LOADS[j][0]) * HD
+            raw = raws[(j, c)][:, :, off : off + w]
+            g = grp.tile([P, w, 4], BF16, name="g%d_%d" % (k, c), tag="grouped", align_bytes=64)
+            st[k]["g"][c] = g
+            halves = raw[:, :, 0 : nr * HD].rearrange("p t (h s c i) -> p s h c t i", s=2, c=16, i=4)
+            share = min(VSHARE[k][c], nr)
+            for s in range(2):
+                dst = g[:, s * rw : (s + 1) * rw, :].rearrange("p (h c i) t -> p h c t i", c=16, i=4)
+                cut = share if s == 0 else 0
+                if cut > 0:
+                    nc.vector.tensor_copy(out=dst[:, 0:cut], in_=halves[:, s, 0:cut])
+                if cut < nr:
+                    nc.scalar.copy(out=dst[:, cut:nr], in_=halves[:, s, cut:nr])
+            if nr < nh:
+                nc.scalar.copy(
+                    out=g[:, 2 * rw : w, :].rearrange("p (c i) t -> p c t i", i=4),
+                    in_=raw[:, :, nr * HD : w].rearrange("p t (c i) -> p c t i", i=4),
+                )
+
+        def quantise(k, c):
+            s = st[k]
             nc.vector.quantize_mx(
-                out=hcodes[:, c, :].bitcast(FP8X4),
-                scales=hscales[:, c, :],
-                in_=hgs[c // 2][:, c % 2].rearrange("p r j -> p (r j)"),
+                out=s["wc"][:, c, :].bitcast(FP8X4),
+                scales=s["ws"][:, c, :],
+                in_=s["g"][c][:].rearrange("p w j -> p (w j)"),
             )
 
-        codes = {}
-
-        def regroup(i):
-            h0, nh = CHUNKS[i]
-            w = nh * HD
-            nr = min(h0 + nh, ROPE_HEADS) - h0
-            rw = nr * HALF
-            wc = wq.tile([P, PASSES, w], U32, name="wc%d" % i, tag="wc", align_bytes=64)
-            ws = wq.tile([P, PASSES, w], U8, name="ws%d" % i, tag="ws", align_bytes=64)
-            codes[i] = (wc, ws)
-            for c in range(PASSES):
-                raw = raws[(i, c)]
-                g = grp.tile([P, w, 4], BF16, name="g%d_%d" % (i, c), tag="grouped", align_bytes=64)
-                halves = raw[:, :, 0 : nr * HD].rearrange("p t (h s c i) -> p s h c t i", s=2, c=16, i=4)
-                pieces = []
-                for s in range(2):
-                    pieces.append(
-                        (g[:, s * rw : (s + 1) * rw, :].rearrange("p (h c i) t -> p h c t i", c=16, i=4), halves[:, s])
-                    )
-                if nr < nh:
-                    pieces.append(
-                        (
-                            g[:, 2 * rw : w, :].rearrange("p (c i) t -> p c t i", i=4),
-                            raw[:, :, nr * HD : w].rearrange("p t (c i) -> p c t i", i=4),
-                        )
-                    )
-                for s, (dst, src) in enumerate(pieces):
-                    if (c, s) in VECTOR_PIECES[i]:
-                        nc.vector.tensor_copy(out=dst, in_=src)
-                    else:
-                        nc.scalar.copy(out=dst, in_=src)
-                nc.vector.quantize_mx(
-                    out=wc[:, c, :].bitcast(FP8X4),
-                    scales=ws[:, c, :],
-                    in_=g[:].rearrange("p w j -> p (w j)"),
+        def rope_passes(k, r, passes):
+            s = st[k]
+            if r not in s["accb"]:
+                s["accb"][r] = psum.tile([P, T], F32, name="accb%d_%d" % (k, r), tag="accb", bufs=3)
+            cols = slice(P * r, P * (r + 1))
+            for c in passes:
+                nc.tensor.matmul_mx(
+                    out=s["accb"][r][:],
+                    lhsT=s["wc"][:, c, cols].bitcast(FP8X4),
+                    lhsT_scale=s["ws"][:, c, cols],
+                    rhs=hcodes[:, c, :].bitcast(FP8X4),
+                    rhs_scale=hscales[:, c, :],
+                    start=(c == 0),
+                    stop=(c == PASSES - 1),
                 )
 
-        bias_h = bias[:].rearrange("p (h d) -> p h d", d=HD)
-        regroup(0)
-        for i, (h0, nh) in enumerate(CHUNKS):
-            if i + 2 < len(CHUNKS):
-                load_chunk(i + 2)
-            if i + 1 < len(CHUNKS):
-                regroup(i + 1)
+        def rope_products(k, r):
+            s = st[k]
+            gr = UNITS[k][0] // 2 + r
+            uu = uvp.tile([P, T], F32, name="uu%d_%d" % (k, r), tag="uv")
+            vv = uvp.tile([P, T], F32, name="vv%d_%d" % (k, r), tag="uv")
+            acc = s["accb"][r]
+            nc.vector.scalar_tensor_tensor(
+                out=uu[:], in0=acc[:], scalar=b_rope[:, gr : gr + 1], in1=cos_t[:], op0=ADD, op1=MULT
+            )
+            nc.vector.scalar_tensor_tensor(
+                out=vv[:], in0=acc[:], scalar=b_rope[:, gr : gr + 1], in1=sin_t[:], op0=ADD, op1=MULT
+            )
+            s["uv"][r] = (uu, vv)
+
+        def get_z(k):
+            s = st[k]
+            if "z" not in s:
+                s["z"] = zp.tile([P, TT, UNITS[k][1] * HD], F32, name="z%d" % k, tag="z")
+            return s["z"]
+
+        def rope_back(k, r):
+            s = st[k]
+            uu, vv = s["uv"][r]
+            y = psum.tile([P, TT, P], F32, name="y%d_%d" % (k, r), tag="y", bufs=2)
+            for t in range(TT):
+                toks = slice(P * t, P * (t + 1))
+                nc.tensor.matmul(out=y[:, t, :], lhsT=uu[:, toks], rhs=ident[:], start=True, stop=False, is_transpose=True)
+                nc.tensor.matmul(out=y[:, t, :], lhsT=vv[:, toks], rhs=swp[:], start=False, stop=True, is_transpose=True)
+            z = get_z(k)
+            zh = z[:].rearrange("p t (h d) -> p t h d", d=HD)
+            nc.scalar.copy(
+                out=zh[:, :, 2 * r : 2 * r + 2, 0:HALF], in_=y[:].rearrange("p t (h d) -> p t h d", d=HALF)
+            )
+
+        def plain_columns(k, t):
+            s = st[k]
+            h0, nh, j = UNITS[k]
             w = nh * HD
-            nr = min(h0 + nh, ROPE_HEADS) - h0
-            rw = nr * HALF
-            wc, ws = codes[i]
-            us = []
-            for r in range(nr // 2):
-                cols = slice(P * r, P * (r + 1))
-                acc_b = psum.tile([P, T], F32, name="accb%d_%d" % (i, r), tag="accb", bufs=4)
+            rw = rope_heads(k) * HALF
+            z = get_z(k)
+            zt = z[:, t, :]
+            zh = zt.rearrange("p (h d) -> p h d", d=HD)
+            for g0, n in split_widths(w - rw):
+                cols = slice(rw + g0, rw + g0 + n)
+                acc_a = psum.tile([P, 512], F32, name="acca%d_%d_%d" % (k, t, g0), tag="acca", bufs=3)
                 for c in range(PASSES):
                     nc.tensor.matmul_mx(
-                        out=acc_b[:],
-                        lhsT=wc[:, c, cols].bitcast(FP8X4),
-                        lhsT_scale=ws[:, c, cols],
-                        rhs=hcodes[:, c, :].bitcast(FP8X4),
-                        rhs_scale=hscales[:, c, :],
+                        out=acc_a[:, 0:n],
+                        lhsT=hcodes[:, c, P * t : P * (t + 1)].bitcast(FP8X4),
+                        lhsT_scale=hscales[:, c, P * t : P * (t + 1)],
+                        rhs=s["wc"][:, c, cols].bitcast(FP8X4),
+                        rhs_scale=s["ws"][:, c, cols],
                         start=(c == 0),
                         stop=(c == PASSES - 1),
                     )
-                gr = h0 // 2 + r
-                uu = uvp.tile([P, T], F32, name="uu%d_%d" % (i, r), tag="uv")
-                vv = uvp.tile([P, T], F32, name="vv%d_%d" % (i, r), tag="uv")
-                nc.vector.scalar_tensor_tensor(
-                    out=uu[:], in0=acc_b[:], scalar=b_rope[:, gr : gr + 1], in1=cos_t[:], op0=ADD, op1=MULT
-                )
-                nc.vector.scalar_tensor_tensor(
-                    out=vv[:], in0=acc_b[:], scalar=b_rope[:, gr : gr + 1], in1=sin_t[:], op0=ADD, op1=MULT
-                )
-                us.append((uu, vv))
-            zs = []
-            for t in range(TT):
-                z = zp.tile([P, w], F32, name="z%d_%d" % (i, t), tag="z")
-                zs.append(z)
-                zh = z[:].rearrange("p (h d) -> p h d", d=HD)
-                for g0, n in split_widths(w - rw):
-                    cols = slice(rw + g0, rw + g0 + n)
-                    acc_a = psum.tile([P, 512], F32, name="acca%d_%d_%d" % (i, t, g0), tag="acca", bufs=2)
-                    for c in range(PASSES):
-                        nc.tensor.matmul_mx(
-                            out=acc_a[:, 0:n],
-                            lhsT=hcodes[:, c, P * t : P * (t + 1)].bitcast(FP8X4),
-                            lhsT_scale=hscales[:, c, P * t : P * (t + 1)],
-                            rhs=wc[:, c, cols].bitcast(FP8X4),
-                            rhs_scale=ws[:, c, cols],
-                            start=(c == 0),
-                            stop=(c == PASSES - 1),
-                        )
-                    if g0 < rw:
-                        b0, b1 = g0 // HALF, min(g0 + n, rw) // HALF
-                        nc.vector.tensor_tensor(
-                            out=zh[:, b0:b1, HALF:HD],
-                            in0=acc_a[:, 0 : (b1 - b0) * HALF].rearrange("p (h d) -> p h d", d=HALF),
-                            in1=bias_h[:, h0 + b0 : h0 + b1, HALF:HD],
-                            op=ADD,
-                        )
-                    if g0 + n > rw:
-                        v0 = max(g0, rw)
-                        zc = slice(v0 + rw, g0 + n + rw)
-                        nc.vector.tensor_tensor(
-                            out=z[:, zc],
-                            in0=acc_a[:, v0 - g0 : n],
-                            in1=bias[:, h0 * HD + v0 + rw : h0 * HD + g0 + n + rw],
-                            op=ADD,
-                        )
-            for t in range(TT):
-                z = zs[t]
-                zh = z[:].rearrange("p (h d) -> p h d", d=HD)
-                toks = slice(P * t, P * (t + 1))
-                y = psum.tile([P, 512], F32, name="y%d_%d" % (i, t), tag="y", bufs=2)
-                for r, (uu, vv) in enumerate(us):
-                    cols = slice(P * r, P * (r + 1))
-                    nc.tensor.matmul(out=y[:, cols], lhsT=uu[:, toks], rhs=ident[:], start=True, stop=False, is_transpose=True)
-                    nc.tensor.matmul(out=y[:, cols], lhsT=vv[:, toks], rhs=swp[:], start=False, stop=True, is_transpose=True)
-                nc.scalar.copy(out=zh[:, 0:nr, 0:HALF], in_=y[:, 0:rw].rearrange("p (h d) -> p h d", d=HALF))
+                if g0 < rw:
+                    b0, b1 = g0 // HALF, min(g0 + n, rw) // HALF
+                    nc.vector.tensor_tensor(
+                        out=zh[:, b0:b1, HALF:HD],
+                        in0=acc_a[:, 0 : (b1 - b0) * HALF].rearrange("p (h d) -> p h d", d=HALF),
+                        in1=bias_h[:, h0 + b0 : h0 + b1, HALF:HD],
+                        op=ADD,
+                    )
+                if g0 + n > rw:
+                    v0 = max(g0, rw)
+                    nc.vector.tensor_tensor(
+                        out=zt[:, v0 + rw : g0 + n + rw],
+                        in0=acc_a[:, v0 - g0 : n],
+                        in1=bias[:, h0 * HD + v0 + rw : h0 * HD + g0 + n + rw],
+                        op=ADD,
+                    )
+
+        stored = set()
+
+        def store(k, upto):
+            h0, nh, j = UNITS[k]
+            w = nh * HD
+            c0 = h0 * HD
+            z = get_z(k)
+            for t in range(upto + 1):
+                if (k, t) in stored:
+                    continue
+                stored.add((k, t))
                 rows = slice(P * t, P * (t + 1))
-                c0 = h0 * HD
-                qw = min(c0 + w, QS) - c0
-                nc.sync.dma_start(out=q_out[rows, c0 : c0 + qw], in_=z[:, 0:qw])
+                qw = max(min(c0 + w, QS) - c0, 0)
+                if qw > 0:
+                    nc.sync.dma_start(out=q_out[rows, c0 : c0 + qw], in_=z[:, t, 0:qw])
                 if qw < w:
-                    nc.sync.dma_start(out=k_out[rows, :], in_=z[:, qw : qw + KS])
-                    nc.sync.dma_start(out=v_out[rows, :], in_=z[:, qw + KS : qw + 2 * KS])
+                    nc.sync.dma_start(out=k_out[rows, :], in_=z[:, t, qw : qw + KS])
+                    nc.sync.dma_start(out=v_out[rows, :], in_=z[:, t, qw + KS : qw + 2 * KS])
+
+        every = list(range(PASSES))
+        hidden()
+        for c in range(PASSES):
+            if c > 0:
+                quantise(0, c - 1)
+            regroup(0, c)
+
+        quantise(0, PASSES - 1)
+        for k in range(n_units):
+            more = k + 1 < n_units
+            nt = tiles(k)
+            early = min(nt, EARLY) if k > 0 else 0
+            for c in range(PASSES):
+                if more and c > 0:
+                    quantise(k + 1, c - 1)
+                if more:
+                    regroup(k + 1, c)
+                if c == 0:
+                    for r in range(early):
+                        rope_passes(k, r, [PASSES - 1])
+                if c == 0 and k > 0 and tiles(k - 1) == PASSES:
+                    rope_back(k - 1, PASSES - 1)
+                    store(k - 1, TT - 1)
+                if c > 0 and c - 1 < nt:
+                    rope_back(k, c - 1)
+                first = min(nt, early + (1 if early else 2))
+                if c == 0:
+                    for r in range(early, first):
+                        rope_passes(k, r, every)
+                if c == 1:
+                    for r in range(first, nt):
+                        rope_passes(k, r, every)
+                if c < nt:
+                    rope_products(k, c)
+                plain_columns(k, c)
+                if c >= nt:
+                    store(k, c)
+                if c == PASSES - 1 and more:
+                    for r in range(min(tiles(k + 1), EARLY)):
+                        rope_passes(k + 1, r, every[0 : PASSES - 1])
+                load_next()
+            if more:
+                quantise(k + 1, PASSES - 1)
+        if tiles(n_units - 1) == PASSES:
+            rope_back(n_units - 1, PASSES - 1)
+            store(n_units - 1, TT - 1)

@@ -22,18 +22,19 @@ ROPE_HEADS = NQ + NKV
 FLOPS = 2 * T * H * OUT
 
 LOADS = [(0, 4), (4, 8), (12, 8), (20, 8), (28, 8)]
-UNITS = [(0, 4, 0), (4, 8, 1), (12, 8, 2), (20, 8, 3), (28, 4, 4), (32, 4, 4)]
+UNITS = [(0, 4, 0), (4, 8, 1), (12, 8, 2), (20, 8, 3), (28, 6, 4), (34, 2, 4)]
 VSHARE = [[4, 4, 4, 4], [8, 8, 8, 8], [4, 4, 4, 4], [4, 4, 4, 4], [4, 4, 4, 4], [0, 0, 0, 0]]
 HEAD_LOADS = ["hs", 4, "b0", 4, 2, "bias"]
 RAW_SLOTS = 10
 EARLY = 0
 PIN = False
+HEAD_BANKS = [("y", 2), ("y", 2), ("acca", 3), ("acca", 3), ("acca", 3), ("accb", 3), ("accb", 3), ("accb", 3)]
 
 
-def split_widths(width):
+def split_widths(width, sizes=(512, 256, 128)):
     parts = []
     start = 0
-    for n in (512, 256, 128):
+    for n in sizes:
         while width - start >= n:
             parts.append((start, n))
             start += n
@@ -108,32 +109,33 @@ def tile_selfattention_pa_kernel(tc, hidden_states, cos, sin, W_qkv, b_qkv, out_
                 for q in range(item):
                     load_next()
 
-        idv = ident[:].rearrange("p (m e) -> p m e", e=2)
-        swv = swp[:].rearrange("p (m e) -> p m e", e=2)
-        for e in range(2):
-            nc.vector.tensor_copy(out=swv[:, :, e], in_=idv[:, :, 1 - e])
+        def tables():
+            idv = ident[:].rearrange("p (m e) -> p m e", e=2)
+            swv = swp[:].rearrange("p (m e) -> p m e", e=2)
+            for e in range(2):
+                nc.vector.tensor_copy(out=swv[:, :, e], in_=idv[:, :, 1 - e])
 
-        cn = uvp.tile([P, TT, 2, 32, 2], F32, name="cn", tag="uv")
-        sn = uvp.tile([P, TT, 2, 32, 2], F32, name="sn", tag="uv")
-        nc.vector.tensor_scalar_mul(out=sinn[:, :, 0:32], in0=sinn[:, :, 0:32], scalar1=-1.0)
-        for e in range(2):
-            nc.vector.tensor_copy(
-                out=cn[:, :, :, :, e],
-                in_=cosn[:, :, 32 * e : 32 * (e + 1)].unsqueeze(2).to_broadcast([P, TT, 2, 32]),
-            )
-            nc.vector.tensor_copy(
-                out=sn[:, :, :, :, e],
-                in_=sinn[:, :, 32 * (1 - e) : 32 * (2 - e)].unsqueeze(2).to_broadcast([P, TT, 2, 32]),
-            )
-        nc.vector.tensor_copy(out=browf[:], in_=brow[:])
-        for src, dst in ((cn, cos_t), (sn, sin_t)):
-            tb = psum.tile([P, T], F32, name="tb", tag="y", bufs=2)
-            for t in range(TT):
-                nc.tensor.transpose(tb[:, P * t : P * (t + 1)], src[:, t].rearrange("p h j e -> p (h j e)"), ident[:])
-            nc.vector.tensor_copy(out=dst[:], in_=tb[:])
-        pb = psum.tile([P, T], F32, name="pb", tag="y", bufs=2)
-        nc.tensor.transpose(pb[:, 0:P], browf[:], ident[:])
-        nc.vector.tensor_copy(out=b_rope[:], in_=pb[:, 0 : ROPE_HEADS // 2])
+            cn = uvp.tile([P, TT, 2, 32, 2], F32, name="cn", tag="uv")
+            sn = uvp.tile([P, TT, 2, 32, 2], F32, name="sn", tag="uv")
+            nc.vector.tensor_scalar_mul(out=sinn[:, :, 0:32], in0=sinn[:, :, 0:32], scalar1=-1.0)
+            for e in range(2):
+                nc.vector.tensor_copy(
+                    out=cn[:, :, :, :, e],
+                    in_=cosn[:, :, 32 * e : 32 * (e + 1)].unsqueeze(2).to_broadcast([P, TT, 2, 32]),
+                )
+                nc.vector.tensor_copy(
+                    out=sn[:, :, :, :, e],
+                    in_=sinn[:, :, 32 * (1 - e) : 32 * (2 - e)].unsqueeze(2).to_broadcast([P, TT, 2, 32]),
+                )
+            nc.vector.tensor_copy(out=browf[:], in_=brow[:])
+            for src, dst in ((cn, cos_t), (sn, sin_t)):
+                tb = psum.tile([P, T], F32, name="tb", tag="y", bufs=2)
+                for t in range(TT):
+                    nc.tensor.transpose(tb[:, P * t : P * (t + 1)], src[:, t].rearrange("p h j e -> p (h j e)"), ident[:])
+                nc.vector.tensor_copy(out=dst[:], in_=tb[:])
+            pb = psum.tile([P, T], F32, name="pb", tag="y", bufs=2)
+            nc.tensor.transpose(pb[:, 0:P], browf[:], ident[:])
+            nc.vector.tensor_copy(out=b_rope[:], in_=pb[:, 0 : ROPE_HEADS // 2])
 
         def hidden():
             hgs = []
@@ -143,13 +145,14 @@ def tile_selfattention_pa_kernel(tc, hidden_states, cos, sin, W_qkv, b_qkv, out_
             for t in range(TT):
                 xw = x_all[:, t, :].bitcast(F32)
                 for cp in range(2):
-                    xt = psum.tile([P, 2, 2, P], F32, name="xt%d_%d" % (t, cp), tag="y", bufs=2)
+                    tag, bufs = HEAD_BANKS[2 * t + cp]
+                    xt = psum.tile([P, 2, 2, P], F32, name="xt%d_%d" % (t, cp), tag=tag, bufs=bufs)
                     for ci in range(2):
                         c = 2 * cp + ci
                         for u in range(2):
                             nc.tensor.transpose(xt[:, ci, u, :], xw[:, 256 * c + u : 256 * (c + 1) : 2], ident[:])
                     dst = hgs[cp][:].bitcast(F32)[:, :, P * t : P * (t + 1), :]
-                    if cp == 9:
+                    if cp == 1:
                         nc.vector.tensor_copy(out=dst, in_=xt[:].rearrange("p c u r -> p c r u"))
                     else:
                         nc.scalar.copy(out=dst, in_=xt[:].rearrange("p c u r -> p c r u"))
@@ -182,9 +185,9 @@ def tile_selfattention_pa_kernel(tc, hidden_states, cos, sin, W_qkv, b_qkv, out_
             raw = raws[(j, c)][:, :, off : off + w]
             g = grp.tile([P, w, 4], BF16, name="g%d_%d" % (k, c), tag="grouped", align_bytes=64)
             st[k]["g"][c] = g
-            halves = raw[:, :, 0 : nr * HD].rearrange("p t (h s c i) -> p s h c t i", s=2, c=16, i=4)
             share = min(VSHARE[k][c], nr)
-            for s in range(2):
+            for s in range(2 if nr > 0 else 0):
+                halves = raw[:, :, 0 : nr * HD].rearrange("p t (h s c i) -> p s h c t i", s=2, c=16, i=4)
                 dst = g[:, s * rw : (s + 1) * rw, :].rearrange("p (h c i) t -> p h c t i", c=16, i=4)
                 cut = share if s == 0 else 0
                 if cut > 0:
@@ -199,11 +202,12 @@ def tile_selfattention_pa_kernel(tc, hidden_states, cos, sin, W_qkv, b_qkv, out_
 
         def quantise(k, c):
             s = st[k]
-            nc.vector.quantize_mx(
-                out=s["wc"][:, c, :].bitcast(FP8X4),
-                scales=s["ws"][:, c, :],
-                in_=s["g"][c][:].rearrange("p w j -> p (w j)"),
-            )
+            for c0, n in split_widths(UNITS[k][1] * HD, (1024, 512, 256, 128)):
+                nc.vector.quantize_mx(
+                    out=s["wc"][:, c, c0 : c0 + n].bitcast(FP8X4),
+                    scales=s["ws"][:, c, c0 : c0 + n],
+                    in_=s["g"][c][:, c0 : c0 + n, :].rearrange("p w j -> p (w j)"),
+                )
 
         def rope_passes(k, r, passes):
             s = st[k]
@@ -305,15 +309,14 @@ def tile_selfattention_pa_kernel(tc, hidden_states, cos, sin, W_qkv, b_qkv, out_
                     continue
                 stored.add((k, t))
                 rows = slice(P * t, P * (t + 1))
-                qw = max(min(c0 + w, QS) - c0, 0)
-                if qw > 0:
-                    nc.sync.dma_start(out=q_out[rows, c0 : c0 + qw], in_=z[:, t, 0:qw])
-                if qw < w:
-                    nc.sync.dma_start(out=k_out[rows, :], in_=z[:, t, qw : qw + KS])
-                    nc.sync.dma_start(out=v_out[rows, :], in_=z[:, t, qw + KS : qw + 2 * KS])
+                for dst, d0, d1 in ((q_out, 0, QS), (k_out, QS, QS + KS), (v_out, QS + KS, OUT)):
+                    a, b = max(c0, d0), min(c0 + w, d1)
+                    if a < b:
+                        nc.sync.dma_start(out=dst[rows, a - d0 : b - d0], in_=z[:, t, a - c0 : b - c0])
 
         every = list(range(PASSES))
         hidden()
+        tables()
         for c in range(PASSES):
             if c > 0:
                 quantise(0, c - 1)

@@ -55,19 +55,21 @@ def tile_selfattention_pa_kernel(tc, hidden_states, cos, sin, W_qkv, b_qkv, out_
         grp = ctx.enter_context(tc.tile_pool(name="grp", bufs=4))
         wq = ctx.enter_context(tc.tile_pool(name="wq", bufs=2))
         zp = ctx.enter_context(tc.tile_pool(name="zp", bufs=2))
-        uvp = ctx.enter_context(tc.tile_pool(name="uvp", bufs=6))
+        uvp = ctx.enter_context(tc.tile_pool(name="uvp", bufs=3))
         psum = ctx.enter_context(tc.psum_pool(name="psum", bufs=1))
 
         ident = const.tile([P, P], F32, name="ident")
         make_identity(nc, ident[:])
         swp = const.tile([P, P], F32, name="swp")
-        cosn = const.tile([P, TT, 64], BF16, name="cosn")
-        sinn = const.tile([P, TT, 64], BF16, name="sinn")
+        identb = const.tile([P, P], BF16, name="identb")
+        sel_c = const.tile([P, P], BF16, name="sel_c")
+        sel_s = const.tile([P, P], BF16, name="sel_s")
+        cs = const.tile([P, TT, P], BF16, name="cs")
+        cs_t = const.tile([P, T], BF16, name="cs_t")
         brow = const.tile([P, P], BF16, name="brow")
         browf = const.tile([P, P], F32, name="browf")
         b_rope = const.tile([P, ROPE_HEADS // 2], F32, name="b_rope")
-        cos_t = const.tile([P, T], BF16, name="cos_t")
-        sin_t = const.tile([P, T], BF16, name="sin_t")
+        cs_rope = const.tile([P, 2, T], BF16, name="cs_rope")
         bias = const.tile([P, OUT], BF16, name="bias")
         hcodes = const.tile([P, PASSES, T], U32, name="hcodes", align_bytes=64)
         hscales = const.tile([P, PASSES, T], U8, name="hscales", align_bytes=64)
@@ -89,8 +91,8 @@ def tile_selfattention_pa_kernel(tc, hidden_states, cos, sin, W_qkv, b_qkv, out_
             raws[(j, c)] = raw
 
         nc.vector.memset(brow[:], 0.0)
-        nc.scalar.dma_start(out=cosn[:], in_=cos.rearrange("(t p) d -> p t d", p=P))
-        nc.scalar.dma_start(out=sinn[:], in_=sin.rearrange("(t p) d -> p t d", p=P))
+        nc.scalar.dma_start(out=cs[:, :, 0:HALF], in_=cos.rearrange("(t p) d -> p t d", p=P))
+        nc.scalar.dma_start(out=cs[:, :, HALF:P], in_=sin.rearrange("(t p) d -> p t d", p=P))
         nc.scalar.dma_start(
             out=brow[0 : ROPE_HEADS // 2, :].rearrange("r (h d) -> r h d", h=2),
             in_=b_qkv[0 : ROPE_HEADS * HD].rearrange("(r h s d) -> r h s d", h=2, s=2, d=HALF)[:, :, 0, :],
@@ -109,30 +111,33 @@ def tile_selfattention_pa_kernel(tc, hidden_states, cos, sin, W_qkv, b_qkv, out_
                 for q in range(item):
                     load_next()
 
-        def tables():
+        def selectors():
             idv = ident[:].rearrange("p (m e) -> p m e", e=2)
             swv = swp[:].rearrange("p (m e) -> p m e", e=2)
             for e in range(2):
                 nc.vector.tensor_copy(out=swv[:, :, e], in_=idv[:, :, 1 - e])
-
-            cn = uvp.tile([P, TT, 2, 32, 2], F32, name="cn", tag="uv")
-            sn = uvp.tile([P, TT, 2, 32, 2], F32, name="sn", tag="uv")
-            nc.vector.tensor_scalar_mul(out=sinn[:, :, 0:32], in0=sinn[:, :, 0:32], scalar1=-1.0)
-            for e in range(2):
-                nc.vector.tensor_copy(
-                    out=cn[:, :, :, :, e],
-                    in_=cosn[:, :, 32 * e : 32 * (e + 1)].unsqueeze(2).to_broadcast([P, TT, 2, 32]),
-                )
-                nc.vector.tensor_copy(
-                    out=sn[:, :, :, :, e],
-                    in_=sinn[:, :, 32 * (1 - e) : 32 * (2 - e)].unsqueeze(2).to_broadcast([P, TT, 2, 32]),
-                )
+            nc.vector.tensor_copy(out=identb[:], in_=ident[:])
+            idx = ident[:].rearrange("p (x e j) -> p x j e", x=2, e=2)
+            nc.vector.tensor_copy(
+                out=sel_c[:].rearrange("p (h j e) -> p h j e", h=2, e=2),
+                in_=idx[:, 0].unsqueeze(1).to_broadcast([P, 2, 32, 2]),
+            )
+            ssv = sel_s[:].rearrange("p (h j e) -> p h j e", h=2, e=2)
+            nc.vector.tensor_copy(out=ssv[:, :, :, 0], in_=idx[:, 1, :, 1].unsqueeze(1).to_broadcast([P, 2, 32]))
+            nc.vector.tensor_scalar_mul(
+                out=ssv[:, :, :, 1], in0=idx[:, 1, :, 0].unsqueeze(1).to_broadcast([P, 2, 32]), scalar1=-1.0
+            )
             nc.vector.tensor_copy(out=browf[:], in_=brow[:])
-            for src, dst in ((cn, cos_t), (sn, sin_t)):
-                tb = psum.tile([P, T], F32, name="tb", tag="y", bufs=2)
-                for t in range(TT):
-                    nc.tensor.transpose(tb[:, P * t : P * (t + 1)], src[:, t].rearrange("p h j e -> p (h j e)"), ident[:])
-                nc.vector.tensor_copy(out=dst[:], in_=tb[:])
+
+        def tables():
+            tp = psum.tile([P, T], BF16, name="tp", tag="y", bufs=2)
+            for t in range(TT):
+                nc.tensor.transpose(tp[:, P * t : P * (t + 1)], cs[:, t, :], identb[:])
+            nc.vector.tensor_copy(out=cs_t[:], in_=tp[:])
+            for x, sel in enumerate((sel_c, sel_s)):
+                tb = psum.tile([P, T], BF16, name="tb", tag="y", bufs=2)
+                nc.tensor.matmul(out=tb[:], lhsT=sel[:], rhs=cs_t[:], start=True, stop=True)
+                nc.vector.tensor_copy(out=cs_rope[:, x, :], in_=tb[:])
             pb = psum.tile([P, T], F32, name="pb", tag="y", bufs=2)
             nc.tensor.transpose(pb[:, 0:P], browf[:], ident[:])
             nc.vector.tensor_copy(out=b_rope[:], in_=pb[:, 0 : ROPE_HEADS // 2])
@@ -228,16 +233,17 @@ def tile_selfattention_pa_kernel(tc, hidden_states, cos, sin, W_qkv, b_qkv, out_
         def rope_products(k, r):
             s = st[k]
             gr = UNITS[k][0] // 2 + r
-            uu = uvp.tile([P, T], F32, name="uu%d_%d" % (k, r), tag="uv")
-            vv = uvp.tile([P, T], F32, name="vv%d_%d" % (k, r), tag="uv")
+            uv = uvp.tile([P, 2, T], F32, name="uv%d_%d" % (k, r), tag="uv")
             acc = s["accb"][r]
             nc.vector.scalar_tensor_tensor(
-                out=uu[:], in0=acc[:], scalar=b_rope[:, gr : gr + 1], in1=cos_t[:], op0=ADD, op1=MULT
+                out=uv[:],
+                in0=acc[:].unsqueeze(1).to_broadcast([P, 2, T]),
+                scalar=b_rope[:, gr : gr + 1],
+                in1=cs_rope[:],
+                op0=ADD,
+                op1=MULT,
             )
-            nc.vector.scalar_tensor_tensor(
-                out=vv[:], in0=acc[:], scalar=b_rope[:, gr : gr + 1], in1=sin_t[:], op0=ADD, op1=MULT
-            )
-            s["uv"][r] = (uu, vv)
+            s["uv"][r] = uv
 
         def get_z(k):
             s = st[k]
@@ -247,12 +253,12 @@ def tile_selfattention_pa_kernel(tc, hidden_states, cos, sin, W_qkv, b_qkv, out_
 
         def rope_back(k, r):
             s = st[k]
-            uu, vv = s["uv"][r]
+            uv = s["uv"][r]
             y = psum.tile([P, TT, P], F32, name="y%d_%d" % (k, r), tag="y", bufs=2)
             for t in range(TT):
                 toks = slice(P * t, P * (t + 1))
-                nc.tensor.matmul(out=y[:, t, :], lhsT=uu[:, toks], rhs=ident[:], start=True, stop=False, is_transpose=True)
-                nc.tensor.matmul(out=y[:, t, :], lhsT=vv[:, toks], rhs=swp[:], start=False, stop=True, is_transpose=True)
+                nc.tensor.matmul(out=y[:, t, :], lhsT=uv[:, 0, toks], rhs=ident[:], start=True, stop=False, is_transpose=True)
+                nc.tensor.matmul(out=y[:, t, :], lhsT=uv[:, 1, toks], rhs=swp[:], start=False, stop=True, is_transpose=True)
             z = get_z(k)
             zh = z[:].rearrange("p t (h d) -> p t h d", d=HD)
             nc.scalar.copy(
@@ -315,6 +321,7 @@ def tile_selfattention_pa_kernel(tc, hidden_states, cos, sin, W_qkv, b_qkv, out_
                         nc.sync.dma_start(out=dst[rows, a - d0 : b - d0], in_=z[:, t, a - c0 : b - c0])
 
         every = list(range(PASSES))
+        selectors()
         hidden()
         tables()
         for c in range(PASSES):

@@ -23,8 +23,8 @@ FLOPS = 2 * T * H * OUT
 
 LOADS = [(0, 4), (4, 8), (12, 8), (20, 8), (28, 8)]
 UNITS = [(0, 4, 0), (4, 8, 1), (12, 8, 2), (20, 8, 3), (28, 6, 4), (34, 2, 4)]
-VSHARE = [[4, 4, 4, 4], [8, 8, 8, 8], [4, 4, 4, 4], [4, 4, 4, 4], [4, 4, 4, 4], [0, 0, 0, 0]]
-HEAD_LOADS = ["hs", 4, "b0", 4, 2, "bias"]
+VSHARE = [[4, 4, 4, 4], [8, 8, 8, 8], [6, 4, 6, 4], [6, 4, 6, 4], [4, 4, 4, 4], [0, 0, 0, 0]]
+HEAD_LOADS = [4, "hs", "small", "b0", 4, 2, "bias"]
 RAW_SLOTS = 10
 EARLY = 0
 PIN = False
@@ -91,18 +91,19 @@ def tile_selfattention_pa_kernel(tc, hidden_states, cos, sin, W_qkv, b_qkv, out_
             raws[(j, c)] = raw
 
         nc.vector.memset(brow[:], 0.0)
-        nc.scalar.dma_start(out=cs[:, :, 0:HALF], in_=cos.rearrange("(t p) d -> p t d", p=P))
-        nc.scalar.dma_start(out=cs[:, :, HALF:P], in_=sin.rearrange("(t p) d -> p t d", p=P))
-        nc.scalar.dma_start(
-            out=brow[0 : ROPE_HEADS // 2, :].rearrange("r (h d) -> r h d", h=2),
-            in_=b_qkv[0 : ROPE_HEADS * HD].rearrange("(r h s d) -> r h s d", h=2, s=2, d=HALF)[:, :, 0, :],
-        )
         x_all = zp.tile([P, TT, H], BF16, name="x_all", tag="z")
         b_cut = UNITS[0][1] * HD
         for item in HEAD_LOADS:
             if item == "hs":
                 for t in range(TT):
                     nc.sync.dma_start(out=x_all[:, t, :], in_=hidden_states[P * t : P * (t + 1), :])
+            elif item == "small":
+                nc.sync.dma_start(out=cs[:, :, 0:HALF], in_=cos.rearrange("(t p) d -> p t d", p=P))
+                nc.sync.dma_start(out=cs[:, :, HALF:P], in_=sin.rearrange("(t p) d -> p t d", p=P))
+                nc.sync.dma_start(
+                    out=brow[0 : ROPE_HEADS // 2, :].rearrange("r (h d) -> r h d", h=2),
+                    in_=b_qkv[0 : ROPE_HEADS * HD].rearrange("(r h s d) -> r h s d", h=2, s=2, d=HALF)[:, :, 0, :],
+                )
             elif item == "b0":
                 nc.sync.dma_start(out=bias[:, 0:b_cut], in_=b_qkv[0:b_cut].partition_broadcast(P))
             elif item == "bias":
@@ -142,6 +143,15 @@ def tile_selfattention_pa_kernel(tc, hidden_states, cos, sin, W_qkv, b_qkv, out_
             nc.tensor.transpose(pb[:, 0:P], browf[:], ident[:])
             nc.vector.tensor_copy(out=b_rope[:], in_=pb[:, 0 : ROPE_HEADS // 2])
 
+        def quantise_hidden(hgs, t):
+            toks = slice(P * t, P * (t + 1))
+            for c in range(PASSES):
+                nc.vector.quantize_mx(
+                    out=hcodes[:, c, toks].bitcast(FP8X4),
+                    scales=hscales[:, c, toks],
+                    in_=hgs[c // 2][:, c % 2, toks, :].rearrange("p r j -> p (r j)"),
+                )
+
         def hidden():
             hgs = []
             for cp in range(2):
@@ -157,16 +167,10 @@ def tile_selfattention_pa_kernel(tc, hidden_states, cos, sin, W_qkv, b_qkv, out_
                         for u in range(2):
                             nc.tensor.transpose(xt[:, ci, u, :], xw[:, 256 * c + u : 256 * (c + 1) : 2], ident[:])
                     dst = hgs[cp][:].bitcast(F32)[:, :, P * t : P * (t + 1), :]
-                    if cp == 1:
-                        nc.vector.tensor_copy(out=dst, in_=xt[:].rearrange("p c u r -> p c r u"))
-                    else:
-                        nc.scalar.copy(out=dst, in_=xt[:].rearrange("p c u r -> p c r u"))
-            for c in range(PASSES):
-                nc.vector.quantize_mx(
-                    out=hcodes[:, c, :].bitcast(FP8X4),
-                    scales=hscales[:, c, :],
-                    in_=hgs[c // 2][:, c % 2].rearrange("p r j -> p (r j)"),
-                )
+                    nc.scalar.copy(out=dst, in_=xt[:].rearrange("p c u r -> p c r u"))
+                if t > 0:
+                    quantise_hidden(hgs, t - 1)
+            quantise_hidden(hgs, TT - 1)
 
         st = {}
 
@@ -322,14 +326,13 @@ def tile_selfattention_pa_kernel(tc, hidden_states, cos, sin, W_qkv, b_qkv, out_
 
         every = list(range(PASSES))
         selectors()
-        hidden()
-        tables()
         for c in range(PASSES):
             if c > 0:
                 quantise(0, c - 1)
             regroup(0, c)
-
         quantise(0, PASSES - 1)
+        hidden()
+        tables()
         for k in range(n_units):
             more = k + 1 < n_units
             nt = tiles(k)

@@ -26,7 +26,7 @@ UNITS = [(0, 4, 0), (4, 8, 1), (12, 8, 2), (20, 8, 3), (28, 6, 4), (34, 2, 4)]
 VSHARE = [[4, 4, 4, 4], [8, 8, 8, 8], [6, 4, 6, 4], [6, 4, 6, 4], [4, 4, 4, 4], [0, 0, 0, 0]]
 HEAD_LOADS = [4, "hs", "small", "b0", 4, 2, "bias"]
 RAW_SLOTS = 10
-EARLY = 0
+EARLY = 2
 PIN = False
 HEAD_BANKS = [("y", 2), ("y", 2), ("acca", 3), ("acca", 3), ("acca", 3), ("accb", 3), ("accb", 3), ("accb", 3)]
 

@@ -28,6 +28,7 @@ HEAD_LOADS = [4, "hs", "small", "b0", 4, 2, "bias"]
 RAW_SLOTS = 10
 EARLY = 2
 PIN = False
+RUN = 8
 HEAD_BANKS = [("y", 2), ("y", 2), ("acca", 3), ("acca", 3), ("acca", 3), ("accb", 3), ("accb", 3), ("accb", 3)]
 
 
@@ -196,8 +197,8 @@ def tile_selfattention_pa_kernel(tc, hidden_states, cos, sin, W_qkv, b_qkv, out_
             st[k]["g"][c] = g
             share = min(VSHARE[k][c], nr)
             for s in range(2 if nr > 0 else 0):
-                halves = raw[:, :, 0 : nr * HD].rearrange("p t (h s c i) -> p s h c t i", s=2, c=16, i=4)
-                dst = g[:, s * rw : (s + 1) * rw, :].rearrange("p (h c i) t -> p h c t i", c=16, i=4)
+                halves = raw[:, :, 0 : nr * HD].rearrange("p t (h s c i) -> p s h c t i", s=2, c=HALF // RUN, i=RUN)
+                dst = g[:, s * rw : (s + 1) * rw, :].rearrange("p (h c i) t -> p h c t i", c=HALF // RUN, i=RUN)
                 cut = share if s == 0 else 0
                 if cut > 0:
                     nc.vector.tensor_copy(out=dst[:, 0:cut], in_=halves[:, s, 0:cut])
@@ -205,8 +206,8 @@ def tile_selfattention_pa_kernel(tc, hidden_states, cos, sin, W_qkv, b_qkv, out_
                     nc.scalar.copy(out=dst[:, cut:nr], in_=halves[:, s, cut:nr])
             if nr < nh:
                 nc.scalar.copy(
-                    out=g[:, 2 * rw : w, :].rearrange("p (c i) t -> p c t i", i=4),
-                    in_=raw[:, :, nr * HD : w].rearrange("p t (c i) -> p c t i", i=4),
+                    out=g[:, 2 * rw : w, :].rearrange("p (c i) t -> p c t i", i=RUN),
+                    in_=raw[:, :, nr * HD : w].rearrange("p t (c i) -> p c t i", i=RUN),
                 )
 
         def quantise(k, c):

@@ -24,7 +24,9 @@ FLOPS = 2 * T * H * OUT
 LOADS = [(0, 4), (4, 8), (12, 8), (20, 8), (28, 8)]
 UNITS = [(0, 4, 0), (4, 8, 1), (12, 8, 2), (20, 8, 3), (28, 6, 4), (34, 2, 4)]
 VSHARE = [[4, 4, 4, 4], [8, 8, 8, 8], [6, 4, 6, 4], [6, 4, 6, 4], [4, 4, 4, 4], [0, 0, 0, 0]]
-HEAD_LOADS = [4, "hs", "small", "b0", 4, 2, "bias"]
+HEAD_LOADS = [1, "small", 3, "hs", 6]
+PLAIN = ROPE_HEADS * HALF + KS
+BROWS = OUT // (2 * HD)
 RAW_SLOTS = 10
 EARLY = 2
 PIN = False
@@ -67,14 +69,14 @@ def tile_selfattention_pa_kernel(tc, hidden_states, cos, sin, W_qkv, b_qkv, out_
         sel_s = const.tile([P, P], BF16, name="sel_s")
         cs = const.tile([P, TT, P], BF16, name="cs")
         cs_t = const.tile([P, T], BF16, name="cs_t")
-        brow = const.tile([P, P], BF16, name="brow")
+        brow = const.tile([P, 2 * HD], BF16, name="brow")
         browf = const.tile([P, P], F32, name="browf")
         b_rope = const.tile([P, ROPE_HEADS // 2], F32, name="b_rope")
         cs_rope = const.tile([P, 2, T], BF16, name="cs_rope")
-        bias = const.tile([P, OUT], BF16, name="bias")
+        bias = const.tile([P, PLAIN], BF16, name="bias")
         hcodes = const.tile([P, PASSES, T], U32, name="hcodes", align_bytes=64)
         hscales = const.tile([P, PASSES, T], U8, name="hscales", align_bytes=64)
-        bias_h = bias[:].rearrange("p (h d) -> p h d", d=HD)
+        brow_s = brow[:].rearrange("r (h s d) -> r s h d", s=2, d=HALF)
 
         raws = {}
         pending = [(j, c) for j in range(len(LOADS)) for c in range(PASSES)]
@@ -93,22 +95,16 @@ def tile_selfattention_pa_kernel(tc, hidden_states, cos, sin, W_qkv, b_qkv, out_
 
         nc.vector.memset(brow[:], 0.0)
         x_all = zp.tile([P, TT, H], BF16, name="x_all", tag="z")
-        b_cut = UNITS[0][1] * HD
         for item in HEAD_LOADS:
             if item == "hs":
                 for t in range(TT):
                     nc.sync.dma_start(out=x_all[:, t, :], in_=hidden_states[P * t : P * (t + 1), :])
             elif item == "small":
-                nc.sync.dma_start(out=cs[:, :, 0:HALF], in_=cos.rearrange("(t p) d -> p t d", p=P))
-                nc.sync.dma_start(out=cs[:, :, HALF:P], in_=sin.rearrange("(t p) d -> p t d", p=P))
-                nc.sync.dma_start(
-                    out=brow[0 : ROPE_HEADS // 2, :].rearrange("r (h d) -> r h d", h=2),
-                    in_=b_qkv[0 : ROPE_HEADS * HD].rearrange("(r h s d) -> r h s d", h=2, s=2, d=HALF)[:, :, 0, :],
-                )
-            elif item == "b0":
-                nc.sync.dma_start(out=bias[:, 0:b_cut], in_=b_qkv[0:b_cut].partition_broadcast(P))
-            elif item == "bias":
-                nc.sync.dma_start(out=bias[:, b_cut:OUT], in_=b_qkv[b_cut:OUT].partition_broadcast(P))
+                nc.sync.dma_start(out=cs[:, :, 0:HALF], in_=cos.rearrange("(p t) d -> p t d", t=TT))
+                nc.sync.dma_start(out=cs[:, :, HALF:P], in_=sin.rearrange("(p t) d -> p t d", t=TT))
+                b_rows = b_qkv.rearrange("(r w) -> r w", w=2 * HD)
+                nc.sync.dma_start(out=brow[0:16, :], in_=b_rows[0:16, :])
+                nc.sync.dma_start(out=brow[16:BROWS, :], in_=b_rows[16:BROWS, :])
             else:
                 for q in range(item):
                     load_next()
@@ -129,13 +125,15 @@ def tile_selfattention_pa_kernel(tc, hidden_states, cos, sin, W_qkv, b_qkv, out_
             nc.vector.tensor_scalar_mul(
                 out=ssv[:, :, :, 1], in0=idx[:, 1, :, 0].unsqueeze(1).to_broadcast([P, 2, 32]), scalar1=-1.0
             )
-            nc.vector.tensor_copy(out=browf[:], in_=brow[:])
+            nc.vector.tensor_copy(out=browf[:].rearrange("r (h d) -> r h d", d=HALF), in_=brow_s[:, 0])
 
         def tables():
             tp = psum.tile([P, T], BF16, name="tp", tag="y", bufs=2)
             for t in range(TT):
                 nc.tensor.transpose(tp[:, P * t : P * (t + 1)], cs[:, t, :], identb[:])
-            nc.vector.tensor_copy(out=cs_t[:], in_=tp[:])
+            nc.vector.tensor_copy(
+                out=cs_t[:].rearrange("k (p t) -> k p t", t=TT), in_=tp[:].rearrange("k (t p) -> k p t", t=TT)
+            )
             for x, sel in enumerate((sel_c, sel_s)):
                 tb = psum.tile([P, T], BF16, name="tb", tag="y", bufs=2)
                 nc.tensor.matmul(out=tb[:], lhsT=sel[:], rhs=cs_t[:], start=True, stop=True)
@@ -143,6 +141,26 @@ def tile_selfattention_pa_kernel(tc, hidden_states, cos, sin, W_qkv, b_qkv, out_
             pb = psum.tile([P, T], F32, name="pb", tag="y", bufs=2)
             nc.tensor.transpose(pb[:, 0:P], browf[:], ident[:])
             nc.vector.tensor_copy(out=b_rope[:], in_=pb[:, 0 : ROPE_HEADS // 2])
+            for b0 in range(0, PLAIN, 1024):
+                bw = min(1024, PLAIN - b0)
+                sp = psum.tile([P, 1024], BF16, name="sp%d" % b0, tag="acca", bufs=3)
+                for r in range(b0 // HD, min((b0 + bw) // HD, ROPE_HEADS // 2)):
+                    nc.tensor.matmul(
+                        out=sp[:, r * HD - b0 : (r + 1) * HD - b0].rearrange("p (h d) -> p h d", d=HALF),
+                        lhsT=identb[:, r : r + 1].to_broadcast([P, P]),
+                        rhs=brow_s[:, 1],
+                        start=True,
+                        stop=True,
+                    )
+                if b0 + bw == PLAIN:
+                    nc.tensor.matmul(
+                        out=sp[:, bw - KS : bw],
+                        lhsT=identb[:, BROWS - 1 : BROWS].to_broadcast([P, P]),
+                        rhs=brow[:],
+                        start=True,
+                        stop=True,
+                    )
+                nc.scalar.copy(out=bias[:, b0 : b0 + bw], in_=sp[:, 0:bw])
 
         def quantise_hidden(hgs, t):
             toks = slice(P * t, P * (t + 1))
@@ -296,7 +314,7 @@ def tile_selfattention_pa_kernel(tc, hidden_states, cos, sin, W_qkv, b_qkv, out_
                     nc.vector.tensor_tensor(
                         out=zh[:, b0:b1, HALF:HD],
                         in0=acc_a[:, 0 : (b1 - b0) * HALF].rearrange("p (h d) -> p h d", d=HALF),
-                        in1=bias_h[:, h0 + b0 : h0 + b1, HALF:HD],
+                        in1=bias[:, (h0 + b0) * HALF : (h0 + b1) * HALF].rearrange("p (h d) -> p h d", d=HALF),
                         op=ADD,
                     )
                 if g0 + n > rw:
@@ -304,7 +322,7 @@ def tile_selfattention_pa_kernel(tc, hidden_states, cos, sin, W_qkv, b_qkv, out_
                     nc.vector.tensor_tensor(
                         out=zt[:, v0 + rw : g0 + n + rw],
                         in0=acc_a[:, v0 - g0 : n],
-                        in1=bias[:, h0 * HD + v0 + rw : h0 * HD + g0 + n + rw],
+                        in1=bias[:, h0 * HALF + v0 : h0 * HALF + g0 + n],
                         op=ADD,
                     )
 

@@ -24,10 +24,10 @@ FLOPS = 2 * T * H * OUT
 LOADS = [(0, 4), (4, 8), (12, 8), (20, 8), (28, 8)]
 UNITS = [(0, 4, 0), (4, 8, 1), (12, 8, 2), (20, 8, 3), (28, 6, 4), (34, 2, 4)]
 VSHARE = [[4, 4, 4, 4], [8, 8, 8, 8], [6, 4, 6, 4], [6, 4, 6, 4], [4, 4, 4, 4], [0, 0, 0, 0]]
-HEAD_LOADS = [1, "small", 3, "hs", 6]
+HEAD_LOADS = [1, "small", 3, "hs", 5]
 PLAIN = ROPE_HEADS * HALF + KS
 BROWS = OUT // (2 * HD)
-RAW_SLOTS = 10
+RAW_SLOTS = 9
 EARLY = 2
 PIN = False
 RUN = 8
@@ -57,7 +57,7 @@ def tile_selfattention_pa_kernel(tc, hidden_states, cos, sin, W_qkv, b_qkv, out_
         rawp = ctx.enter_context(tc.tile_pool(name="rawp", bufs=RAW_SLOTS))
         grp = ctx.enter_context(tc.tile_pool(name="grp", bufs=4))
         wq = ctx.enter_context(tc.tile_pool(name="wq", bufs=2))
-        zp = ctx.enter_context(tc.tile_pool(name="zp", bufs=2))
+        zp = ctx.enter_context(tc.tile_pool(name="zp", bufs=3))
         uvp = ctx.enter_context(tc.tile_pool(name="uvp", bufs=3))
         psum = ctx.enter_context(tc.psum_pool(name="psum", bufs=1))
 
@@ -343,6 +343,9 @@ def tile_selfattention_pa_kernel(tc, hidden_states, cos, sin, W_qkv, b_qkv, out_
                     if a < b:
                         nc.sync.dma_start(out=dst[rows, a - d0 : b - d0], in_=z[:, t, a - c0 : b - c0])
 
+        def at_step(c, nt):
+            return [r for r in range(nt) if [0, 1, 1, 2][r] == c]
+
         every = list(range(PASSES))
         selectors()
         for c in range(PASSES):
@@ -364,11 +367,8 @@ def tile_selfattention_pa_kernel(tc, hidden_states, cos, sin, W_qkv, b_qkv, out_
                 if c == 0:
                     for r in range(early):
                         rope_passes(k, r, [PASSES - 1])
-                if c == 0 and k > 0 and tiles(k - 1) == PASSES:
-                    rope_back(k - 1, PASSES - 1)
-                    store(k - 1, TT - 1)
-                if c > 0 and c - 1 < nt:
-                    rope_back(k, c - 1)
+                for r in at_step(c - 1, nt):
+                    rope_back(k, r)
                 first = min(nt, early + (1 if early else 2))
                 if c == 0:
                     for r in range(early, first):
@@ -376,10 +376,12 @@ def tile_selfattention_pa_kernel(tc, hidden_states, cos, sin, W_qkv, b_qkv, out_
                 if c == 1:
                     for r in range(first, nt):
                         rope_passes(k, r, every)
-                if c < nt:
-                    rope_products(k, c)
+                for r in at_step(c, nt):
+                    rope_products(k, r)
+                if c == PASSES - 1:
+                    store(k, c - 1)
                 plain_columns(k, c)
-                if c >= nt:
+                if c == PASSES - 1:
                     store(k, c)
                 if c == PASSES - 1 and more:
                     for r in range(min(tiles(k + 1), EARLY)):
@@ -387,6 +389,3 @@ def tile_selfattention_pa_kernel(tc, hidden_states, cos, sin, W_qkv, b_qkv, out_
                 load_next()
             if more:
                 quantise(k + 1, PASSES - 1)
-        if tiles(n_units - 1) == PASSES:
-            rope_back(n_units - 1, PASSES - 1)
-            store(n_units - 1, TT - 1)

@@ -168,13 +168,13 @@ def tile_selfattention_pa_kernel(tc, hidden_states, cos, sin, W_qkv, b_qkv, out_
                 nc.vector.quantize_mx(
                     out=hcodes[:, c, toks].bitcast(FP8X4),
                     scales=hscales[:, c, toks],
-                    in_=hgs[c // 2][:, c % 2, toks, :].rearrange("p r j -> p (r j)"),
+                    in_=hgs[c // 2][:, t, c % 2, :, :].rearrange("p r j -> p (r j)"),
                 )
 
         def hidden():
             hgs = []
             for cp in range(2):
-                hg = grp.tile([P, 2, T, 4], BF16, name="hg%d" % cp, tag="grouped", align_bytes=64)
+                hg = grp.tile([P, TT, 2, P, 4], BF16, name="hg%d" % cp, tag="grouped", align_bytes=64)
                 hgs.append(hg)
             for t in range(TT):
                 xw = x_all[:, t, :].bitcast(F32)
@@ -185,7 +185,7 @@ def tile_selfattention_pa_kernel(tc, hidden_states, cos, sin, W_qkv, b_qkv, out_
                         c = 2 * cp + ci
                         for u in range(2):
                             nc.tensor.transpose(xt[:, ci, u, :], xw[:, 256 * c + u : 256 * (c + 1) : 2], ident[:])
-                    dst = hgs[cp][:].bitcast(F32)[:, :, P * t : P * (t + 1), :]
+                    dst = hgs[cp][:].bitcast(F32)[:, t]
                     nc.scalar.copy(out=dst, in_=xt[:].rearrange("p c u r -> p c r u"))
                 if t > 0:
                     quantise_hidden(hgs, t - 1)
@@ -296,33 +296,38 @@ def tile_selfattention_pa_kernel(tc, hidden_states, cos, sin, W_qkv, b_qkv, out_
             z = get_z(k)
             zt = z[:, t, :]
             zh = zt.rearrange("p (h d) -> p h d", d=HD)
-            for g0, n in split_widths(w - rw):
-                cols = slice(rw + g0, rw + g0 + n)
-                acc_a = psum.tile([P, 512], F32, name="acca%d_%d_%d" % (k, t, g0), tag="acca", bufs=3)
-                for c in range(PASSES):
-                    nc.tensor.matmul_mx(
-                        out=acc_a[:, 0:n],
-                        lhsT=hcodes[:, c, P * t : P * (t + 1)].bitcast(FP8X4),
-                        lhsT_scale=hscales[:, c, P * t : P * (t + 1)],
-                        rhs=s["wc"][:, c, cols].bitcast(FP8X4),
-                        rhs_scale=s["ws"][:, c, cols],
-                        start=(c == 0),
-                        stop=(c == PASSES - 1),
-                    )
-                if g0 < rw:
-                    b0, b1 = g0 // HALF, min(g0 + n, rw) // HALF
+            for b0 in range(0, w - rw, 512):
+                bw = min(512, w - rw - b0)
+                tag = "acca" if rw > 0 or t < PASSES - 1 else "accb"
+                acc_a = psum.tile([P, 512], F32, name="acca%d_%d_%d" % (k, t, b0), tag=tag, bufs=3)
+                for g0, n in split_widths(bw):
+                    cols = slice(rw + b0 + g0, rw + b0 + g0 + n)
+                    for c in range(PASSES):
+                        nc.tensor.matmul_mx(
+                            out=acc_a[:, g0 : g0 + n],
+                            lhsT=hcodes[:, c, P * t : P * (t + 1)].bitcast(FP8X4),
+                            lhsT_scale=hscales[:, c, P * t : P * (t + 1)],
+                            rhs=s["wc"][:, c, cols].bitcast(FP8X4),
+                            rhs_scale=s["ws"][:, c, cols],
+                            start=(c == 0),
+                            stop=(c == PASSES - 1),
+                        )
+                rb = min(bw, rw - b0)
+                if rb > 0:
+                    h_a, h_b = b0 // HALF, (b0 + rb) // HALF
                     nc.vector.tensor_tensor(
-                        out=zh[:, b0:b1, HALF:HD],
-                        in0=acc_a[:, 0 : (b1 - b0) * HALF].rearrange("p (h d) -> p h d", d=HALF),
-                        in1=bias[:, (h0 + b0) * HALF : (h0 + b1) * HALF].rearrange("p (h d) -> p h d", d=HALF),
+                        out=zh[:, h_a:h_b, HALF:HD],
+                        in0=acc_a[:, 0:rb].rearrange("p (h d) -> p h d", d=HALF),
+                        in1=bias[:, h0 * HALF + b0 : h0 * HALF + b0 + rb].rearrange("p (h d) -> p h d", d=HALF),
                         op=ADD,
                     )
-                if g0 + n > rw:
-                    v0 = max(g0, rw)
+                else:
+                    rb = 0
+                if rb < bw:
                     nc.vector.tensor_tensor(
-                        out=zt[:, v0 + rw : g0 + n + rw],
-                        in0=acc_a[:, v0 - g0 : n],
-                        in1=bias[:, h0 * HALF + v0 : h0 * HALF + g0 + n],
+                        out=zt[:, rw + b0 + rb : rw + b0 + bw],
+                        in0=acc_a[:, rb:bw],
+                        in1=bias[:, h0 * HALF + b0 + rb : h0 * HALF + b0 + bw],
                         op=ADD,
                     )
 

from contextlib import ExitStack

import concourse.mybir as mybir
from concourse.masks import make_identity

F32 = mybir.dt.float32
BF16 = mybir.dt.bfloat16
U32 = mybir.dt.uint32
U8 = mybir.dt.uint8
FP8X4 = mybir.dt.float8_e4m3fn_x4
ADD = mybir.AluOpType.add
MULT = mybir.AluOpType.mult

P = 128
T, H, NQ, NKV, HD = 512, 2048, 32, 2, 128
QS, KS = NQ * HD, NKV * HD
OUT = QS + 2 * KS
PASSES = H // 512
TT = T // P
HALF = HD // 2
ROPE_HEADS = NQ + NKV
FLOPS = 2 * T * H * OUT

LOADS = [(0, 4), (4, 8), (12, 8), (20, 8), (28, 8)]
UNITS = [(0, 4, 0), (4, 8, 1), (12, 8, 2), (20, 8, 3), (28, 6, 4), (34, 2, 4)]
VSHARE = [[4, 4, 4, 4], [8, 8, 8, 8], [6, 4, 6, 4], [6, 4, 6, 4], [4, 4, 4, 4], [0, 0, 0, 0]]
HEAD_LOADS = [1, "small", 3, "hs", 5]
PLAIN = ROPE_HEADS * HALF + KS
BROWS = OUT // (2 * HD)
RAW_SLOTS = 9
EARLY = 2
PIN = False
RUN = 8
HEAD_BANKS = [("y", 2), ("y", 2), ("acca", 3), ("acca", 3), ("acca", 3), ("accb", 3), ("accb", 3), ("accb", 3)]


def split_widths(width, sizes=(512, 256, 128)):
    parts = []
    start = 0
    for n in sizes:
        while width - start >= n:
            parts.append((start, n))
            start += n
    return parts


def tile_selfattention_pa_kernel(tc, hidden_states, cos, sin, W_qkv, b_qkv, out_0, out_1, out_2):
    nc = tc.nc
    q_out = out_0.rearrange("t h d -> t (h d)")
    k_out = out_1.rearrange("t h d -> t (h d)")
    v_out = out_2.rearrange("t h d -> t (h d)")
    n_units = len(UNITS)
    with ExitStack() as ctx:
        if PIN:
            ctx.enter_context(tc.manual_schedule())
        const = ctx.enter_context(tc.tile_pool(name="const", bufs=1))
        rawp = ctx.enter_context(tc.tile_pool(name="rawp", bufs=RAW_SLOTS))
        grp = ctx.enter_context(tc.tile_pool(name="grp", bufs=4))
        wq = ctx.enter_context(tc.tile_pool(name="wq", bufs=2))
        zp = ctx.enter_context(tc.tile_pool(name="zp", bufs=3))
        uvp = ctx.enter_context(tc.tile_pool(name="uvp", bufs=3))
        psum = ctx.enter_context(tc.psum_pool(name="psum", bufs=1))

        ident = const.tile([P, P], F32, name="ident")
        make_identity(nc, ident[:])
        swp = const.tile([P, P], F32, name="swp")
        identb = const.tile([P, P], BF16, name="identb")
        sel_c = const.tile([P, P], BF16, name="sel_c")
        sel_s = const.tile([P, P], BF16, name="sel_s")
        cs = const.tile([P, TT, P], BF16, name="cs")
        cs_t = const.tile([P, T], BF16, name="cs_t")
        brow = const.tile([P, 2 * HD], BF16, name="brow")
        browf = const.tile([P, P], F32, name="browf")
        b_rope = const.tile([P, ROPE_HEADS // 2], F32, name="b_rope")
        cs_rope = const.tile([P, 2, T], BF16, name="cs_rope")
        bias = const.tile([P, PLAIN], BF16, name="bias")
        hcodes = const.tile([P, PASSES, T], U32, name="hcodes", align_bytes=64)
        hscales = const.tile([P, PASSES, T], U8, name="hscales", align_bytes=64)
        brow_s = brow[:].rearrange("r (h s d) -> r s h d", s=2, d=HALF)

        raws = {}
        pending = [(j, c) for j in range(len(LOADS)) for c in range(PASSES)]

        def load_next():
            if not pending:
                return
            j, c = pending.pop(0)
            h0, nh = LOADS[j]
            raw = rawp.tile([P, 4, nh * HD], BF16, name="raw%d_%d" % (j, c), tag="raw")
            nc.sync.dma_start(
                out=raw[:],
                in_=W_qkv[512 * c : 512 * (c + 1), h0 * HD : (h0 + nh) * HD].rearrange("(p j) w -> p j w", j=4),
            )
            raws[(j, c)] = raw

        nc.vector.memset(brow[:], 0.0)
        x_all = zp.tile([P, TT, H], BF16, name="x_all", tag="z")
        for item in HEAD_LOADS:
            if item == "hs":
                for t in range(TT):
                    nc.sync.dma_start(out=x_all[:, t, :], in_=hidden_states[P * t : P * (t + 1), :])
            elif item == "small":
                nc.sync.dma_start(out=cs[:, :, 0:HALF], in_=cos.rearrange("(p t) d -> p t d", t=TT))
                nc.sync.dma_start(out=cs[:, :, HALF:P], in_=sin.rearrange("(p t) d -> p t d", t=TT))
                b_rows = b_qkv.rearrange("(r w) -> r w", w=2 * HD)
                nc.sync.dma_start(out=brow[0:16, :], in_=b_rows[0:16, :])
                nc.sync.dma_start(out=brow[16:BROWS, :], in_=b_rows[16:BROWS, :])
            else:
                for q in range(item):
                    load_next()

        def selectors():
            idv = ident[:].rearrange("p (m e) -> p m e", e=2)
            swv = swp[:].rearrange("p (m e) -> p m e", e=2)
            for e in range(2):
                nc.vector.tensor_copy(out=swv[:, :, e], in_=idv[:, :, 1 - e])
            nc.vector.tensor_copy(out=identb[:], in_=ident[:])
            idx = ident[:].rearrange("p (x e j) -> p x j e", x=2, e=2)
            nc.vector.tensor_copy(
                out=sel_c[:].rearrange("p (h j e) -> p h j e", h=2, e=2),
                in_=idx[:, 0].unsqueeze(1).to_broadcast([P, 2, 32, 2]),
            )
            ssv = sel_s[:].rearrange("p (h j e) -> p h j e", h=2, e=2)
            nc.vector.tensor_copy(out=ssv[:, :, :, 0], in_=idx[:, 1, :, 1].unsqueeze(1).to_broadcast([P, 2, 32]))
            nc.vector.tensor_scalar_mul(
                out=ssv[:, :, :, 1], in0=idx[:, 1, :, 0].unsqueeze(1).to_broadcast([P, 2, 32]), scalar1=-1.0
            )
            nc.vector.tensor_copy(out=browf[:].rearrange("r (h d) -> r h d", d=HALF), in_=brow_s[:, 0])

        def tables():
            tp = psum.tile([P, T], BF16, name="tp", tag="y", bufs=2)
            for t in range(TT):
                nc.tensor.transpose(tp[:, P * t : P * (t + 1)], cs[:, t, :], identb[:])
            nc.vector.tensor_copy(
                out=cs_t[:].rearrange("k (p t) -> k p t", t=TT), in_=tp[:].rearrange("k (t p) -> k p t", t=TT)
            )
            for x, sel in enumerate((sel_c, sel_s)):
                tb = psum.tile([P, T], BF16, name="tb", tag="y", bufs=2)
                nc.tensor.matmul(out=tb[:], lhsT=sel[:], rhs=cs_t[:], start=True, stop=True)
                nc.vector.tensor_copy(out=cs_rope[:, x, :], in_=tb[:])
            pb = psum.tile([P, T], F32, name="pb", tag="y", bufs=2)
            nc.tensor.transpose(pb[:, 0:P], browf[:], ident[:])
            nc.vector.tensor_copy(out=b_rope[:], in_=pb[:, 0 : ROPE_HEADS // 2])
            for b0 in range(0, PLAIN, 1024):
                bw = min(1024, PLAIN - b0)
                sp = psum.tile([P, 1024], BF16, name="sp%d" % b0, tag="acca", bufs=3)
                for r in range(b0 // HD, min((b0 + bw) // HD, ROPE_HEADS // 2)):
                    nc.tensor.matmul(
                        out=sp[:, r * HD - b0 : (r + 1) * HD - b0].rearrange("p (h d) -> p h d", d=HALF),
                        lhsT=identb[:, r : r + 1].to_broadcast([P, P]),
                        rhs=brow_s[:, 1],
                        start=True,
                        stop=True,
                    )
                if b0 + bw == PLAIN:
                    nc.tensor.matmul(
                        out=sp[:, bw - KS : bw],
                        lhsT=identb[:, BROWS - 1 : BROWS].to_broadcast([P, P]),
                        rhs=brow[:],
                        start=True,
                        stop=True,
                    )
                nc.scalar.copy(out=bias[:, b0 : b0 + bw], in_=sp[:, 0:bw])

        def quantise_hidden(hgs, t):
            toks = slice(P * t, P * (t + 1))
            for c in range(PASSES):
                nc.vector.quantize_mx(
                    out=hcodes[:, c, toks].bitcast(FP8X4),
                    scales=hscales[:, c, toks],
                    in_=hgs[c // 2][:, t, c % 2, :, :].rearrange("p r j -> p (r j)"),
                )

        def hidden():
            hgs = []
            for cp in range(2):
                hg = grp.tile([P, TT, 2, P, 4], BF16, name="hg%d" % cp, tag="grouped", align_bytes=64)
                hgs.append(hg)
            for t in range(TT):
                xw = x_all[:, t, :].bitcast(F32)
                for cp in range(2):
                    tag, bufs = HEAD_BANKS[2 * t + cp]
                    xt = psum.tile([P, 2, 2, P], F32, name="xt%d_%d" % (t, cp), tag=tag, bufs=bufs)
                    for ci in range(2):
                        c = 2 * cp + ci
                        for u in range(2):
                            nc.tensor.transpose(xt[:, ci, u, :], xw[:, 256 * c + u : 256 * (c + 1) : 2], ident[:])
                    dst = hgs[cp][:].bitcast(F32)[:, t]
                    nc.scalar.copy(out=dst, in_=xt[:].rearrange("p c u r -> p c r u"))
                if t > 0:
                    quantise_hidden(hgs, t - 1)
            quantise_hidden(hgs, TT - 1)

        st = {}

        def rope_heads(k):
            h0, nh, j = UNITS[k]
            return min(h0 + nh, ROPE_HEADS) - h0

        def tiles(k):
            return rope_heads(k) // 2

        def regroup(k, c):
            h0, nh, j = UNITS[k]
            w = nh * HD
            nr = rope_heads(k)
            rw = nr * HALF
            if c == 0:
                wc = wq.tile([P, PASSES, w], U32, name="wc%d" % k, tag="wc", align_bytes=64)
                ws = wq.tile([P, PASSES, w], U8, name="ws%d" % k, tag="ws", align_bytes=64)
                st[k] = {"wc": wc, "ws": ws, "g": {}, "accb": {}, "uv": {}, "y": {}, "acca": {}}
            off = (h0 - LOADS[j][0]) * HD
            raw = raws[(j, c)][:, :, off : off + w]
            g = grp.tile([P, w, 4], BF16, name="g%d_%d" % (k, c), tag="grouped", align_bytes=64)
            st[k]["g"][c] = g
            share = min(VSHARE[k][c], nr)
            for s in range(2 if nr > 0 else 0):
                halves = raw[:, :, 0 : nr * HD].rearrange("p t (h s c i) -> p s h c t i", s=2, c=HALF // RUN, i=RUN)
                dst = g[:, s * rw : (s + 1) * rw, :].rearrange("p (h c i) t -> p h c t i", c=HALF // RUN, i=RUN)
                cut = share if s == 0 else 0
                if cut > 0:
                    nc.vector.tensor_copy(out=dst[:, 0:cut], in_=halves[:, s, 0:cut])
                if cut < nr:
                    nc.scalar.copy(out=dst[:, cut:nr], in_=halves[:, s, cut:nr])
            if nr < nh:
                nc.scalar.copy(
                    out=g[:, 2 * rw : w, :].rearrange("p (c i) t -> p c t i", i=RUN),
                    in_=raw[:, :, nr * HD : w].rearrange("p t (c i) -> p c t i", i=RUN),
                )

        def quantise(k, c):
            s = st[k]
            for c0, n in split_widths(UNITS[k][1] * HD, (1024, 512, 256, 128)):
                nc.vector.quantize_mx(
                    out=s["wc"][:, c, c0 : c0 + n].bitcast(FP8X4),
                    scales=s["ws"][:, c, c0 : c0 + n],
                    in_=s["g"][c][:, c0 : c0 + n, :].rearrange("p w j -> p (w j)"),
                )

        def rope_passes(k, r, passes):
            s = st[k]
            if r not in s["accb"]:
                s["accb"][r] = psum.tile([P, T], F32, name="accb%d_%d" % (k, r), tag="accb", bufs=3)
            cols = slice(P * r, P * (r + 1))
            for c in passes:
                nc.tensor.matmul_mx(
                    out=s["accb"][r][:],
                    lhsT=s["wc"][:, c, cols].bitcast(FP8X4),
                    lhsT_scale=s["ws"][:, c, cols],
                    rhs=hcodes[:, c, :].bitcast(FP8X4),
                    rhs_scale=hscales[:, c, :],
                    start=(c == 0),
                    stop=(c == PASSES - 1),
                )

        def rope_products(k, r):
            s = st[k]
            gr = UNITS[k][0] // 2 + r
            uv = uvp.tile([P, 2, T], F32, name="uv%d_%d" % (k, r), tag="uv")
            acc = s["accb"][r]
            nc.vector.scalar_tensor_tensor(
                out=uv[:],
                in0=acc[:].unsqueeze(1).to_broadcast([P, 2, T]),
                scalar=b_rope[:, gr : gr + 1],
                in1=cs_rope[:],
                op0=ADD,
                op1=MULT,
            )
            s["uv"][r] = uv

        def get_z(k):
            s = st[k]
            if "z" not in s:
                s["z"] = zp.tile([P, TT, UNITS[k][1] * HD], F32, name="z%d" % k, tag="z")
            return s["z"]

        def rope_back(k, r):
            s = st[k]
            uv = s["uv"][r]
            y = psum.tile([P, TT, P], F32, name="y%d_%d" % (k, r), tag="y", bufs=2)
            for t in range(TT):
                toks = slice(P * t, P * (t + 1))
                nc.tensor.matmul(out=y[:, t, :], lhsT=uv[:, 0, toks], rhs=ident[:], start=True, stop=False, is_transpose=True)
                nc.tensor.matmul(out=y[:, t, :], lhsT=uv[:, 1, toks], rhs=swp[:], start=False, stop=True, is_transpose=True)
            z = get_z(k)
            zh = z[:].rearrange("p t (h d) -> p t h d", d=HD)
            nc.scalar.copy(
                out=zh[:, :, 2 * r : 2 * r + 2, 0:HALF], in_=y[:].rearrange("p t (h d) -> p t h d", d=HALF)
            )

        def plain_columns(k, t):
            s = st[k]
            h0, nh, j = UNITS[k]
            w = nh * HD
            rw = rope_heads(k) * HALF
            z = get_z(k)
            zt = z[:, t, :]
            zh = zt.rearrange("p (h d) -> p h d", d=HD)
            for b0 in range(0, w - rw, 512):
                bw = min(512, w - rw - b0)
                tag = "acca" if rw > 0 or t < PASSES - 1 else "accb"
                acc_a = psum.tile([P, 512], F32, name="acca%d_%d_%d" % (k, t, b0), tag=tag, bufs=3)
                for g0, n in split_widths(bw):
                    cols = slice(rw + b0 + g0, rw + b0 + g0 + n)
                    for c in range(PASSES):
                        nc.tensor.matmul_mx(
                            out=acc_a[:, g0 : g0 + n],
                            lhsT=hcodes[:, c, P * t : P * (t + 1)].bitcast(FP8X4),
                            lhsT_scale=hscales[:, c, P * t : P * (t + 1)],
                            rhs=s["wc"][:, c, cols].bitcast(FP8X4),
                            rhs_scale=s["ws"][:, c, cols],
                            start=(c == 0),
                            stop=(c == PASSES - 1),
                        )
                rb = min(bw, rw - b0)
                if rb > 0:
                    h_a, h_b = b0 // HALF, (b0 + rb) // HALF
                    nc.vector.tensor_tensor(
                        out=zh[:, h_a:h_b, HALF:HD],
                        in0=acc_a[:, 0:rb].rearrange("p (h d) -> p h d", d=HALF),
                        in1=bias[:, h0 * HALF + b0 : h0 * HALF + b0 + rb].rearrange("p (h d) -> p h d", d=HALF),
                        op=ADD,
                    )
                else:
                    rb = 0
                if rb < bw:
                    nc.vector.tensor_tensor(
                        out=zt[:, rw + b0 + rb : rw + b0 + bw],
                        in0=acc_a[:, rb:bw],
                        in1=bias[:, h0 * HALF + b0 + rb : h0 * HALF + b0 + bw],
                        op=ADD,
                    )

        stored = set()

        def store(k, upto):
            h0, nh, j = UNITS[k]
            w = nh * HD
            c0 = h0 * HD
            z = get_z(k)
            for t in range(upto + 1):
                if (k, t) in stored:
                    continue
                stored.add((k, t))
                rows = slice(P * t, P * (t + 1))
                for dst, d0, d1 in ((q_out, 0, QS), (k_out, QS, QS + KS), (v_out, QS + KS, OUT)):
                    a, b = max(c0, d0), min(c0 + w, d1)
                    if a < b:
                        nc.sync.dma_start(out=dst[rows, a - d0 : b - d0], in_=z[:, t, a - c0 : b - c0])

        def at_step(c, nt):
            return [r for r in range(nt) if [0, 1, 1, 2][r] == c]

        every = list(range(PASSES))
        selectors()
        for c in range(PASSES):
            if c > 0:
                quantise(0, c - 1)
            regroup(0, c)
        quantise(0, PASSES - 1)
        hidden()
        tables()
        for k in range(n_units):
            more = k + 1 < n_units
            nt = tiles(k)
            early = min(nt, EARLY) if k > 0 else 0
            for c in range(PASSES):
                if more and c > 0:
                    quantise(k + 1, c - 1)
                if more:
                    regroup(k + 1, c)
                if c == 0:
                    for r in range(early):
                        rope_passes(k, r, [PASSES - 1])
                for r in at_step(c - 1, nt):
                    rope_back(k, r)
                first = min(nt, early + (1 if early else 2))
                if c == 0:
                    for r in range(early, first):
                        rope_passes(k, r, every)
                if c == 1:
                    for r in range(first, nt):
                        rope_passes(k, r, every)
                for r in at_step(c, nt):
                    rope_products(k, r)
                if c == PASSES - 1:
                    store(k, c - 1)
                plain_columns(k, c)
                if c == PASSES - 1:
                    store(k, c)
                if c == PASSES - 1 and more:
                    for r in range(min(tiles(k + 1), EARLY)):
                        rope_passes(k + 1, r, every[0 : PASSES - 1])
                load_next()
            if more:
                quantise(k + 1, PASSES - 1)
